import numpy as np
import ml_dtypes


def mxq(x, axis, fmt="e4m3"):
    dtype, down = {"e4m3": (ml_dtypes.float8_e4m3fn, 7), "e5m2": (ml_dtypes.float8_e5m2, 14)}[fmt]
    v = np.moveaxis(np.asarray(x, np.float32).astype(ml_dtypes.bfloat16).astype(np.float64), axis, -1)
    blocks = v.reshape(v.shape[:-1] + (-1, 32))
    amax = np.abs(blocks).max(-1, keepdims=True)
    byte = np.maximum(np.where(amax > 0, np.frexp(amax)[1] - 1 + 127, 0) - down, 1)
    scale = np.exp2(byte - 127.0)
    codes = (blocks / scale).astype(np.float32).astype(dtype).astype(np.float64)
    return np.moveaxis((codes * scale).reshape(v.shape), -1, axis)


WIDE = False


def mx_kscale(k):
    if not WIDE:
        return np.ones(k)
    levels = np.array([10, -10, 5, -5, 0])
    a = np.random.permutation(np.resize(levels, k // 512 * 4)).reshape(k // 512, 4)
    idx = np.arange(k)
    return np.exp2(a[idx // 512, idx % 128 // 32])


BF16 = ml_dtypes.bfloat16


def bf(x):
    return np.asarray(x, np.float32).astype(BF16)


def f64(x):
    return np.asarray(x).astype(np.float64)


E2M1 = np.array([0.0, 0.5, 1.0, 1.5, 2.0, 3.0, 4.0, 6.0, -0.0, -0.5, -1.0, -1.5, -2.0, -3.0, -4.0, -6.0])


def pack_weight(w, fmt):
    k, n = w.shape
    w = f64(bf(w)).reshape(k // 32, 32, n)
    amax = np.abs(w).max(1)
    if fmt == "e4m3":
        byte = np.frexp(amax)[1] - 1 + 127 - 7
    else:
        mant, ex = np.frexp(amax / 6.0)
        byte = np.where(mant > 0.5, ex, ex - 1) + 127
    byte = np.clip(np.where(amax > 0, byte, 1), 1, 254)
    scaled = (w * np.exp2(127.0 - byte)[:, None, :]).reshape(k, n).astype(np.float32)
    by_word = np.ascontiguousarray(scaled.reshape(k // 512, 128, 4, n).transpose(0, 1, 3, 2))
    if fmt == "e4m3":
        words = by_word.astype(ml_dtypes.float8_e4m3fn).view(np.uint8)
    else:
        c = by_word.astype(ml_dtypes.float4_e2m1fn).view(np.uint8) & 0xF
        words = c[..., 0::2] | (c[..., 1::2] << 4)
    return np.ascontiguousarray(words), np.ascontiguousarray(byte.astype(np.uint8).reshape(k // 512, 16, n))


def unpack_weight(words, scales, fmt):
    g, p, n, _ = words.shape
    if fmt == "e4m3":
        vals = np.ascontiguousarray(words).view(ml_dtypes.float8_e4m3fn).astype(np.float64)
    else:
        nib = np.empty((g, p, n, 4), np.uint8)
        nib[..., 0::2] = words & 0xF
        nib[..., 1::2] = words >> 4
        vals = E2M1[nib]
    vals = vals * np.repeat(np.exp2(scales.astype(np.float64) - 127.0), 8, axis=1)[..., None]
    return vals.transpose(0, 1, 3, 2).reshape(g * 512, n)


B, C, HID, H, W = 2, 1024, 64, 32, 32
N_P, N_H, N_F, N_U, N_L = 7, 3, 2, 4, 2
EPS = 1e-5
FMT = "e4m3"


def setup_inputs():
    s = mx_kscale(C)
    off = 0.5 * np.random.standard_normal((1, C, 1, 1))
    p_nodes = bf(np.random.standard_normal((N_P, B, HID, H, W)))
    h_nodes = bf(np.random.standard_normal((N_H, B, HID, H, W)))
    f_nodes = bf(np.random.standard_normal((N_F, B, HID, H, W)))
    xp = bf((np.random.standard_normal((B, C, H, W)) + off) * s[None, :, None, None])
    h_att = bf(np.random.uniform(0.0, 1.0, (N_H, B, 1, H, W)))
    wu = np.random.standard_normal((N_U * HID, C)) / np.sqrt(C) / s[None, :]
    wl = np.random.standard_normal((N_L * HID, C)) / np.sqrt(C) / s[None, :]
    Wu_words, Wu_scales = pack_weight(np.ascontiguousarray(wu.T), FMT)
    Wl_words, Wl_scales = pack_weight(np.ascontiguousarray(wl.T), FMT)
    return {
        "p_nodes": p_nodes,
        "h_nodes": h_nodes,
        "f_nodes": f_nodes,
        "xp": xp,
        "h_att": h_att,
        "Wu_words": Wu_words,
        "Wu_scales": Wu_scales,
        "Wl_words": Wl_words,
        "Wl_scales": Wl_scales,
        "gamma_u": bf(1.0 + 0.1 * np.random.standard_normal(N_U * HID)),
        "beta_u": bf(0.1 * np.random.standard_normal(N_U * HID)),
        "gamma_l": bf(1.0 + 0.1 * np.random.standard_normal(N_L * HID)),
        "beta_l": bf(0.1 * np.random.standard_normal(N_L * HID)),
    }


def conv_bn_relu(x, Wc, gamma, beta):
    y = (Wc @ mxq(x, 1, "e4m3").reshape(B, C, H * W)).reshape(B, -1, H, W)
    m = y.mean(axis=(0, 2, 3), keepdims=True)
    v = y.var(axis=(0, 2, 3), keepdims=True)
    y = (y - m) / np.sqrt(v + EPS)
    y = y * gamma[None, :, None, None] + beta[None, :, None, None]
    return np.maximum(y, 0.0)


def reference(p_nodes, h_nodes, f_nodes, xp, h_att, Wu_words, Wu_scales, Wl_words, Wl_scales, gamma_u, beta_u, gamma_l, beta_l):
    p_nodes, h_nodes, xp, h_att = f64(p_nodes), f64(h_nodes), f64(xp), f64(h_att)
    du = conv_bn_relu(h_att[1] * xp, unpack_weight(Wu_words, Wu_scales, FMT).T, f64(gamma_u), f64(beta_u))
    dl = conv_bn_relu(h_att[2] * xp, unpack_weight(Wl_words, Wl_scales, FMT).T, f64(gamma_l), f64(beta_l))
    du4 = du.reshape(B, N_U, HID, H, W).transpose(1, 0, 2, 3, 4)
    dl2 = dl.reshape(B, N_L, HID, H, W).transpose(1, 0, 2, 3, 4)
    p0 = 0.5 * (h_nodes[0] + p_nodes[0])
    p_up = 0.5 * (p_nodes[1:1 + N_U] + du4)
    p_low = 0.5 * (p_nodes[1 + N_U:N_P] + dl2)
    return np.concatenate([p0[None], p_up, p_low], axis=0)

@@ -1,0 +1,262 @@
+from contextlib import ExitStack
+
+import concourse.mybir as mybir
+from concourse.masks import make_identity
+
+F32 = mybir.dt.float32
+BF16 = mybir.dt.bfloat16
+I32 = mybir.dt.int32
+U32 = mybir.dt.uint32
+U8 = mybir.dt.uint8
+FP8X4 = mybir.dt.float8_e4m3fn_x4
+ALU = mybir.AluOpType
+ACT = mybir.ActivationFunctionType
+
+P = 128
+PACK = 4
+K_PASS = P * PACK
+IMAGES = 2
+CHANNELS = 1024
+PASSES = CHANNELS // K_PASS
+HID = 64
+PIXELS = 32 * 32
+N_TILE = 512
+PIXEL_TILES = PIXELS // N_TILE
+UPPER, LOWER = 0, 1
+PAIRS_OF = {UPPER: (0, 1), LOWER: (2,)}
+N_PAIRS = 3
+OUT_CHANNELS = N_PAIRS * P
+QUADRANTS = 4
+STATS = 6
+EPS = 1e-5
+
+FLOPS = 2 * OUT_CHANNELS * CHANNELS * IMAGES * PIXELS
+BYTES = (
+    2 * (7 + 1) * IMAGES * HID * PIXELS
+    + 2 * IMAGES * CHANNELS * PIXELS
+    + 2 * 2 * IMAGES * PIXELS
+    + OUT_CHANNELS * CHANNELS + OUT_CHANNELS * CHANNELS // 32
+    + 2 * 2 * OUT_CHANNELS
+    + 4 * 7 * IMAGES * HID * PIXELS
+)
+
+
+def tile_gnn_kernel(
+    tc, p_nodes, h_nodes, f_nodes, xp, h_att,
+    Wu_words, Wu_scales, Wl_words, Wl_scales,
+    gamma_u, beta_u, gamma_l, beta_l, out,
+):
+    nc = tc.nc
+    with ExitStack() as stack:
+        keep = stack.enter_context(tc.tile_pool(name="keep", bufs=1))
+        products = stack.enter_context(tc.tile_pool(name="products", bufs=3))
+        quantised = stack.enter_context(tc.tile_pool(name="quantised", bufs=4))
+        results = stack.enter_context(tc.tile_pool(name="results", bufs=3))
+        psum = stack.enter_context(tc.psum_pool(name="psum", bufs=8))
+
+        affine_rows = keep.tile([P, P], BF16)
+        nc.vector.memset(affine_rows[:].bitcast(I32), 0)
+        att_row = keep.tile([P, 2, IMAGES, PIXELS], BF16)
+        for b in range(IMAGES):
+            for product in (UPPER, LOWER):
+                nc.vector.memset(att_row[:, product, b].bitcast(I32), 0)
+        ones = keep.tile([P, P], BF16)
+        nc.vector.memset(ones[:], 1.0)
+        w_scales = keep.tile([P, PASSES, OUT_CHANNELS], U8, align_bytes=64)
+        nc.vector.memset(w_scales[:].rearrange("p g n -> p (g n)").bitcast(I32), 0)
+        eps = keep.tile([P, 1], F32)
+        nc.vector.memset(eps[:], EPS)
+        identity = keep.tile([P, P], BF16)
+        make_identity(nc, identity[:])
+        table_warmer = keep.tile([P, 1], F32)
+        nc.scalar.activation(out=table_warmer[:], in_=eps[:], func=ACT.Sqrt)
+
+        nc.scalar.dma_start(out=affine_rows[0:2, :], in_=gamma_u.rearrange("(r c) -> r c", c=P))
+        nc.scalar.dma_start(out=affine_rows[2:3, :], in_=gamma_l.rearrange("(r c) -> r c", c=P))
+        nc.scalar.dma_start(out=affine_rows[3:5, :], in_=beta_u.rearrange("(r c) -> r c", c=P))
+        nc.scalar.dma_start(out=affine_rows[5:6, :], in_=beta_l.rearrange("(r c) -> r c", c=P))
+        for scales, first, width in ((Wu_scales, 0, 2 * P), (Wl_scales, 2 * P, P)):
+            for quadrant in range(QUADRANTS):
+                nc.gpsimd.dma_start(
+                    out=w_scales[32 * quadrant : 32 * quadrant + 4, :, first : first + width].bitcast(F32),
+                    in_=scales[:, 4 * quadrant : 4 * quadrant + 4, :].rearrange("g r n -> r g n").bitcast(F32),
+                )
+
+        xp_rows = keep.tile([P, IMAGES, PASSES, PACK, PIXELS], BF16)
+        w_words = keep.tile([P, PASSES, OUT_CHANNELS], U32, align_bytes=64)
+
+        def load_attention(product, b):
+            nc.sync.dma_start(out=att_row[0:1, product, b], in_=h_att[1 + product, b].rearrange("o h w -> o (h w)"))
+
+        def load_pixels(b, wt):
+            for g in range(PASSES):
+                nc.sync.dma_start(
+                    out=xp_rows[:, b, g, :, wt * N_TILE : (wt + 1) * N_TILE],
+                    in_=xp[b, g * K_PASS : (g + 1) * K_PASS].rearrange("(p t) h w -> p t (h w)", t=PACK)[
+                        :, :, wt * N_TILE : (wt + 1) * N_TILE
+                    ],
+                )
+
+        load_attention(UPPER, 0)
+        load_pixels(0, 0)
+        load_attention(LOWER, 0)
+        load_pixels(0, 1)
+        nc.sync.dma_start(
+            out=w_words[:, :, 0 : 2 * P].bitcast(I32),
+            in_=Wu_words.rearrange("g p n t -> p g (n t)").bitcast(I32),
+        )
+        nc.sync.dma_start(
+            out=w_words[:, :, 2 * P : 3 * P].bitcast(I32),
+            in_=Wl_words.rearrange("g p n t -> p g (n t)").bitcast(I32),
+        )
+        load_attention(UPPER, 1)
+        load_attention(LOWER, 1)
+        load_pixels(1, 0)
+        load_pixels(1, 1)
+        h0 = keep.tile([P, PIXELS], BF16)
+        p0 = keep.tile([P, PIXELS], BF16)
+        nc.sync.dma_start(out=h0[:], in_=h_nodes[0].rearrange("b c h w -> (b c) (h w)"))
+        nc.sync.dma_start(out=p0[:], in_=p_nodes[0].rearrange("b c h w -> (b c) (h w)"))
+        p_pairs = keep.tile([P, N_PAIRS, IMAGES, PIXELS], BF16)
+        for pair in range(N_PAIRS):
+            for half in range(2):
+                nc.sync.dma_start(
+                    out=p_pairs[half * HID : (half + 1) * HID, pair],
+                    in_=p_nodes[1 + 2 * pair + half].rearrange("b c h w -> c b (h w)"),
+                )
+
+        affine_ps = psum.tile([P, P], BF16, tag="bank")
+        nc.tensor.transpose(out=affine_ps[:], in_=affine_rows[:], identity=identity[:])
+        affine = keep.tile([P, 2 * N_PAIRS], F32)
+        nc.vector.tensor_copy(out=affine[:], in_=affine_ps[:, 0 : 2 * N_PAIRS])
+
+        att_banks = {}
+        for b in range(IMAGES):
+            for product in (UPPER, LOWER):
+                for wt in range(PIXEL_TILES):
+                    att_ps = psum.tile([P, N_TILE], F32, tag="bank")
+                    nc.tensor.matmul(
+                        out=att_ps[:], lhsT=ones[:], rhs=att_row[:, product, b, wt * N_TILE : (wt + 1) * N_TILE],
+                        start=True, stop=True,
+                    )
+                    att_banks[(product, b, wt)] = att_ps
+        att_pairs = keep.tile([P, 2, IMAGES, PIXELS, 2], BF16)
+
+        def write_attention_pairs(copy, product, b):
+            for wt in range(PIXEL_TILES):
+                copy(
+                    out=att_pairs[:, product, b, wt * N_TILE : (wt + 1) * N_TILE, :],
+                    in_=att_banks[(product, b, wt)][:].unsqueeze(2).to_broadcast([P, N_TILE, 2]),
+                )
+
+        xp_grouped = keep.tile([P, IMAGES, PASSES, PIXELS, PACK], BF16)
+
+        def regroup(b, wt):
+            cols = slice(wt * N_TILE, (wt + 1) * N_TILE)
+            for g in range(PASSES):
+                nc.scalar.copy(
+                    out=xp_grouped[:, b, g, cols, :].rearrange("p (c i) t -> p c t i", i=4),
+                    in_=xp_rows[:, b, g, :, cols].rearrange("p t (c i) -> p c t i", i=4),
+                )
+
+        y_banks = {}
+        stats = keep.tile([P, N_PAIRS, IMAGES * PIXEL_TILES, STATS], F32)
+
+        def convolve(product, b, wt):
+            cols = slice(wt * N_TILE, (wt + 1) * N_TILE)
+            weighted = products.tile([P, PASSES, N_TILE, PACK], BF16, align_bytes=64)
+            for g in range(PASSES):
+                nc.vector.tensor_tensor(
+                    out=weighted[:, g].rearrange("p w (u e) -> p w u e", e=2),
+                    in0=xp_grouped[:, b, g, cols, :].rearrange("p w (u e) -> p w u e", e=2),
+                    in1=att_pairs[:, product, b, cols, :].unsqueeze(2).to_broadcast([P, N_TILE, 2, 2]),
+                    op=ALU.mult,
+                )
+            codes = quantised.tile([P, PASSES * N_TILE], U32, align_bytes=64)
+            scales = quantised.tile([P, PASSES * N_TILE], U8, align_bytes=64)
+            nc.vector.quantize_mx(
+                out=codes[:].bitcast(FP8X4),
+                scales=scales[:],
+                in_=weighted[:].rearrange("p g w t -> p (g w t)"),
+            )
+            for pair in PAIRS_OF[product]:
+                y = psum.tile([P, N_TILE], F32, tag="bank")
+                for g in range(PASSES):
+                    nc.tensor.matmul_mx(
+                        out=y[:],
+                        lhsT=w_words[:, g, pair * P : (pair + 1) * P].bitcast(FP8X4),
+                        lhsT_scale=w_scales[:, g, pair * P : (pair + 1) * P],
+                        rhs=codes[:, g * N_TILE : (g + 1) * N_TILE].bitcast(FP8X4),
+                        rhs_scale=scales[:, g * N_TILE : (g + 1) * N_TILE],
+                        start=(g == 0),
+                        stop=(g == PASSES - 1),
+                    )
+                nc.vector.bn_stats(out=stats[:, pair, b * PIXEL_TILES + wt, :], in_=y[:])
+                y_banks[(pair, b, wt)] = y
+
+        mean_var = keep.tile([P, N_PAIRS, 2], F32)
+        std = keep.tile([P, N_PAIRS], F32)
+        inv_std = keep.tile([P, N_PAIRS], F32)
+        gain = keep.tile([P, N_PAIRS], F32)
+        mean_gain = keep.tile([P, N_PAIRS], F32)
+        shift = keep.tile([P, N_PAIRS], F32)
+
+        def finish(product):
+            pairs = PAIRS_OF[product]
+            these = slice(pairs[0], pairs[-1] + 1)
+            for pair in pairs:
+                nc.vector.bn_aggr(out=mean_var[:, pair, :], in_=stats[:, pair].rearrange("p u s -> p (u s)"))
+            nc.scalar.activation(out=std[:, these], in_=mean_var[:, these, 1], func=ACT.Sqrt, bias=eps[:])
+            nc.vector.reciprocal(out=inv_std[:, these], in_=std[:, these])
+            nc.vector.scalar_tensor_tensor(
+                out=gain[:, these], in0=affine[:, these], scalar=0.5, in1=inv_std[:, these],
+                op0=ALU.mult, op1=ALU.mult,
+            )
+            nc.vector.tensor_tensor(
+                out=mean_gain[:, these], in0=mean_var[:, these, 0], in1=gain[:, these], op=ALU.mult
+            )
+            nc.vector.scalar_tensor_tensor(
+                out=shift[:, these], in0=affine[:, N_PAIRS + pairs[0] : N_PAIRS + pairs[-1] + 1], scalar=0.5,
+                in1=mean_gain[:, these], op0=ALU.mult, op1=ALU.subtract,
+            )
+            for b in range(IMAGES):
+                for pair in pairs:
+                    result = results.tile([P, PIXELS], F32)
+                    for wt in range(PIXEL_TILES):
+                        cols = slice(wt * N_TILE, (wt + 1) * N_TILE)
+                        half_relu = results.tile([P, N_TILE], F32)
+                        nc.scalar.activation(
+                            out=half_relu[:], in_=y_banks[(pair, b, wt)][:], func=ACT.Relu,
+                            bias=shift[:, pair : pair + 1], scale=gain[:, pair : pair + 1],
+                        )
+                        nc.vector.scalar_tensor_tensor(
+                            out=result[:, cols], in0=p_pairs[:, pair, b, cols], scalar=0.5, in1=half_relu[:],
+                            op0=ALU.mult, op1=ALU.add,
+                        )
+                    for half in range(2):
+                        nc.sync.dma_start(
+                            out=out[1 + 2 * pair + half, b].rearrange("c h w -> c (h w)"),
+                            in_=result[half * HID : (half + 1) * HID, :],
+                        )
+
+        for b in range(IMAGES):
+            write_attention_pairs(nc.vector.tensor_copy, UPPER, b)
+            for wt in range(PIXEL_TILES):
+                regroup(b, wt)
+                if wt == 0:
+                    write_attention_pairs(nc.scalar.copy, LOWER, b)
+                convolve(UPPER, b, wt)
+
+        half_h0 = keep.tile([P, PIXELS], F32)
+        nc.scalar.mul(out=half_h0[:], in_=h0[:], mul=0.5)
+        node0 = keep.tile([P, PIXELS], F32)
+        nc.vector.scalar_tensor_tensor(
+            out=node0[:], in0=p0[:], scalar=0.5, in1=half_h0[:], op0=ALU.mult, op1=ALU.add
+        )
+        nc.sync.dma_start(out=out[0].rearrange("b c h w -> (b c) (h w)"), in_=node0[:])
+
+        finish(UPPER)
+        for b in range(IMAGES):
+            for wt in range(PIXEL_TILES):
+                convolve(LOWER, b, wt)
+        finish(LOWER)

@@ -48,33 +48,35 @@ def tile_gnn_kernel(
 ):
     nc = tc.nc
     with ExitStack() as stack:
+        stack.enter_context(tc.manual_schedule())
         keep = stack.enter_context(tc.tile_pool(name="keep", bufs=1))
         products = stack.enter_context(tc.tile_pool(name="products", bufs=3))
-        quantised = stack.enter_context(tc.tile_pool(name="quantised", bufs=4))
+        quantised = stack.enter_context(tc.tile_pool(name="quantised", bufs=1))
         results = stack.enter_context(tc.tile_pool(name="results", bufs=3))
         psum = stack.enter_context(tc.psum_pool(name="psum", bufs=8))
 
-        affine_rows = keep.tile([P, P], BF16)
-        nc.vector.memset(affine_rows[:].bitcast(I32), 0)
         att_row = keep.tile([P, 2, IMAGES, PIXELS], BF16)
-        for b in range(IMAGES):
-            for product in (UPPER, LOWER):
-                nc.vector.memset(att_row[:, product, b].bitcast(I32), 0)
-        ones = keep.tile([P, P], BF16)
-        nc.vector.memset(ones[:], 1.0)
+        affine_rows = keep.tile([P, P], BF16)
         w_scales = keep.tile([P, PASSES, OUT_CHANNELS], U8, align_bytes=64)
-        nc.vector.memset(w_scales[:].rearrange("p g n -> p (g n)").bitcast(I32), 0)
         eps = keep.tile([P, 1], F32)
+        ones = keep.tile([P, P], BF16)
+        nc.vector.memset(att_row[:, UPPER, 0].bitcast(I32), 0)
         nc.vector.memset(eps[:], EPS)
+        nc.vector.memset(affine_rows[:].bitcast(I32), 0)
+        nc.vector.memset(w_scales[:].rearrange("p g n -> p (g n)").bitcast(I32), 0)
+        nc.vector.memset(ones[:], 1.0)
+        nc.vector.memset(att_row[:, LOWER, 0].bitcast(I32), 0)
+        nc.vector.memset(att_row[:, UPPER, 1].bitcast(I32), 0)
+        nc.vector.memset(att_row[:, LOWER, 1].bitcast(I32), 0)
         identity = keep.tile([P, P], BF16)
         make_identity(nc, identity[:])
-        table_warmer = keep.tile([P, 1], F32)
-        nc.scalar.activation(out=table_warmer[:], in_=eps[:], func=ACT.Sqrt)
 
         nc.scalar.dma_start(out=affine_rows[0:2, :], in_=gamma_u.rearrange("(r c) -> r c", c=P))
         nc.scalar.dma_start(out=affine_rows[2:3, :], in_=gamma_l.rearrange("(r c) -> r c", c=P))
         nc.scalar.dma_start(out=affine_rows[3:5, :], in_=beta_u.rearrange("(r c) -> r c", c=P))
         nc.scalar.dma_start(out=affine_rows[5:6, :], in_=beta_l.rearrange("(r c) -> r c", c=P))
+        table_warmer = keep.tile([P, 1], F32)
+        nc.scalar.activation(out=table_warmer[:], in_=eps[:], func=ACT.Sqrt)
         for scales, first, width in ((Wu_scales, 0, 2 * P), (Wl_scales, 2 * P, P)):
             for quadrant in range(QUADRANTS):
                 nc.gpsimd.dma_start(
@@ -100,6 +102,8 @@ def tile_gnn_kernel(
         load_attention(UPPER, 0)
         load_pixels(0, 0)
         load_attention(LOWER, 0)
+        load_attention(UPPER, 1)
+        load_attention(LOWER, 1)
         load_pixels(0, 1)
         nc.sync.dma_start(
             out=w_words[:, :, 0 : 2 * P].bitcast(I32),
@@ -109,8 +113,6 @@ def tile_gnn_kernel(
             out=w_words[:, :, 2 * P : 3 * P].bitcast(I32),
             in_=Wl_words.rearrange("g p n t -> p g (n t)").bitcast(I32),
         )
-        load_attention(UPPER, 1)
-        load_attention(LOWER, 1)
         load_pixels(1, 0)
         load_pixels(1, 1)
         h0 = keep.tile([P, PIXELS], BF16)
@@ -125,21 +127,18 @@ def tile_gnn_kernel(
                     in_=p_nodes[1 + 2 * pair + half].rearrange("b c h w -> c b (h w)"),
                 )
 
-        affine_ps = psum.tile([P, P], BF16, tag="bank")
-        nc.tensor.transpose(out=affine_ps[:], in_=affine_rows[:], identity=identity[:])
-        affine = keep.tile([P, 2 * N_PAIRS], F32)
-        nc.vector.tensor_copy(out=affine[:], in_=affine_ps[:, 0 : 2 * N_PAIRS])
-
+        attention_sets = [(product, b) for b in range(IMAGES) for product in (UPPER, LOWER)]
         att_banks = {}
-        for b in range(IMAGES):
-            for product in (UPPER, LOWER):
-                for wt in range(PIXEL_TILES):
-                    att_ps = psum.tile([P, N_TILE], F32, tag="bank")
-                    nc.tensor.matmul(
-                        out=att_ps[:], lhsT=ones[:], rhs=att_row[:, product, b, wt * N_TILE : (wt + 1) * N_TILE],
-                        start=True, stop=True,
-                    )
-                    att_banks[(product, b, wt)] = att_ps
+
+        def spread_attention(product, b):
+            for wt in range(PIXEL_TILES):
+                att_ps = psum.tile([P, N_TILE], F32, tag="bank")
+                nc.tensor.matmul(
+                    out=att_ps[:], lhsT=ones[:], rhs=att_row[:, product, b, wt * N_TILE : (wt + 1) * N_TILE],
+                    start=True, stop=True,
+                )
+                att_banks[(product, b, wt)] = att_ps
+
         att_pairs = keep.tile([P, 2, IMAGES, PIXELS, 2], BF16)
 
         def write_attention_pairs(copy, product, b):
@@ -149,6 +148,19 @@ def tile_gnn_kernel(
                     in_=att_banks[(product, b, wt)][:].unsqueeze(2).to_broadcast([P, N_TILE, 2]),
                 )
 
+        spread_attention(*attention_sets[0])
+        spread_attention(*attention_sets[1])
+        write_attention_pairs(nc.vector.tensor_copy, *attention_sets[0])
+
+        affine_ps = psum.tile([P, P], BF16, tag="bank")
+        nc.tensor.transpose(out=affine_ps[:], in_=affine_rows[:], identity=identity[:])
+        affine = keep.tile([P, 2 * N_PAIRS], F32)
+        nc.vector.tensor_copy(out=affine[:], in_=affine_ps[:, 0 : 2 * N_PAIRS])
+
+        spread_attention(*attention_sets[2])
+        spread_attention(*attention_sets[3])
+
+        pixel_tiles = [(b, wt) for b in range(IMAGES) for wt in range(PIXEL_TILES)]
         xp_grouped = keep.tile([P, IMAGES, PASSES, PIXELS, PACK], BF16)
 
         def regroup(b, wt):
@@ -159,26 +171,41 @@ def tile_gnn_kernel(
                     in_=xp_rows[:, b, g, :, cols].rearrange("p t (c i) -> p c t i", i=4),
                 )
 
-        y_banks = {}
-        stats = keep.tile([P, N_PAIRS, IMAGES * PIXEL_TILES, STATS], F32)
+        weighted_tiles = {}
 
-        def convolve(product, b, wt):
+        def weigh(product, b, wt, g):
+            if g == 0:
+                weighted = products.tile([P, PASSES, N_TILE, PACK], BF16, align_bytes=64)
+                weighted_tiles[product] = weighted
             cols = slice(wt * N_TILE, (wt + 1) * N_TILE)
-            weighted = products.tile([P, PASSES, N_TILE, PACK], BF16, align_bytes=64)
-            for g in range(PASSES):
-                nc.vector.tensor_tensor(
-                    out=weighted[:, g].rearrange("p w (u e) -> p w u e", e=2),
-                    in0=xp_grouped[:, b, g, cols, :].rearrange("p w (u e) -> p w u e", e=2),
-                    in1=att_pairs[:, product, b, cols, :].unsqueeze(2).to_broadcast([P, N_TILE, 2, 2]),
-                    op=ALU.mult,
-                )
-            codes = quantised.tile([P, PASSES * N_TILE], U32, align_bytes=64)
-            scales = quantised.tile([P, PASSES * N_TILE], U8, align_bytes=64)
+            nc.vector.tensor_tensor(
+                out=weighted_tiles[product][:, g].rearrange("p w (u e) -> p w u e", e=2),
+                in0=xp_grouped[:, b, g, cols, :].rearrange("p w (u e) -> p w u e", e=2),
+                in1=att_pairs[:, product, b, cols, :].unsqueeze(2).to_broadcast([P, N_TILE, 2, 2]),
+                op=ALU.mult,
+            )
+
+        quantised_tiles = {}
+        places = {UPPER: 2, LOWER: len(pixel_tiles)}
+
+        def quantise(product, b, wt):
+            codes = quantised.tile(
+                [P, PASSES * N_TILE], U32, align_bytes=64, tag="codes%d" % product, bufs=places[product]
+            )
+            scales = quantised.tile(
+                [P, PASSES * N_TILE], U8, align_bytes=64, tag="scales%d" % product, bufs=places[product]
+            )
             nc.vector.quantize_mx(
                 out=codes[:].bitcast(FP8X4),
                 scales=scales[:],
-                in_=weighted[:].rearrange("p g w t -> p (g w t)"),
+                in_=weighted_tiles[product][:].rearrange("p g w t -> p (g w t)"),
             )
+            quantised_tiles[(product, b, wt)] = (codes, scales)
+
+        y_banks = {}
+
+        def convolve(product, b, wt):
+            codes, scales = quantised_tiles[(product, b, wt)]
             for pair in PAIRS_OF[product]:
                 y = psum.tile([P, N_TILE], F32, tag="bank")
                 for g in range(PASSES):
@@ -191,8 +218,13 @@ def tile_gnn_kernel(
                         start=(g == 0),
                         stop=(g == PASSES - 1),
                     )
-                nc.vector.bn_stats(out=stats[:, pair, b * PIXEL_TILES + wt, :], in_=y[:])
                 y_banks[(pair, b, wt)] = y
+
+        stats = keep.tile([P, N_PAIRS, len(pixel_tiles), STATS], F32)
+
+        def take_statistics(product, b, wt):
+            for pair in PAIRS_OF[product]:
+                nc.vector.bn_stats(out=stats[:, pair, b * PIXEL_TILES + wt, :], in_=y_banks[(pair, b, wt)][:])
 
         mean_var = keep.tile([P, N_PAIRS, 2], F32)
         std = keep.tile([P, N_PAIRS], F32)
@@ -201,7 +233,7 @@ def tile_gnn_kernel(
         mean_gain = keep.tile([P, N_PAIRS], F32)
         shift = keep.tile([P, N_PAIRS], F32)
 
-        def finish(product):
+        def gain_and_shift(product):
             pairs = PAIRS_OF[product]
             these = slice(pairs[0], pairs[-1] + 1)
             for pair in pairs:
@@ -219,44 +251,61 @@ def tile_gnn_kernel(
                 out=shift[:, these], in0=affine[:, N_PAIRS + pairs[0] : N_PAIRS + pairs[-1] + 1], scalar=0.5,
                 in1=mean_gain[:, these], op0=ALU.mult, op1=ALU.subtract,
             )
-            for b in range(IMAGES):
-                for pair in pairs:
-                    result = results.tile([P, PIXELS], F32)
-                    for wt in range(PIXEL_TILES):
-                        cols = slice(wt * N_TILE, (wt + 1) * N_TILE)
-                        half_relu = results.tile([P, N_TILE], F32)
-                        nc.scalar.activation(
-                            out=half_relu[:], in_=y_banks[(pair, b, wt)][:], func=ACT.Relu,
-                            bias=shift[:, pair : pair + 1], scale=gain[:, pair : pair + 1],
-                        )
-                        nc.vector.scalar_tensor_tensor(
-                            out=result[:, cols], in0=p_pairs[:, pair, b, cols], scalar=0.5, in1=half_relu[:],
-                            op0=ALU.mult, op1=ALU.add,
-                        )
-                    for half in range(2):
-                        nc.sync.dma_start(
-                            out=out[1 + 2 * pair + half, b].rearrange("c h w -> c (h w)"),
-                            in_=result[half * HID : (half + 1) * HID, :],
-                        )
 
-        for b in range(IMAGES):
-            write_attention_pairs(nc.vector.tensor_copy, UPPER, b)
-            for wt in range(PIXEL_TILES):
-                regroup(b, wt)
-                if wt == 0:
-                    write_attention_pairs(nc.scalar.copy, LOWER, b)
-                convolve(UPPER, b, wt)
+        result_tiles = {}
 
+        def finish_bank(pair, b, wt):
+            if wt == 0:
+                result = results.tile([P, PIXELS], F32)
+                result_tiles[pair] = result
+            cols = slice(wt * N_TILE, (wt + 1) * N_TILE)
+            half_relu = results.tile([P, N_TILE], F32)
+            nc.scalar.activation(
+                out=half_relu[:], in_=y_banks[(pair, b, wt)][:], func=ACT.Relu,
+                bias=shift[:, pair : pair + 1], scale=gain[:, pair : pair + 1],
+            )
+            nc.vector.scalar_tensor_tensor(
+                out=result_tiles[pair][:, cols], in0=p_pairs[:, pair, b, cols], scalar=0.5, in1=half_relu[:],
+                op0=ALU.mult, op1=ALU.add,
+            )
+            if wt == PIXEL_TILES - 1:
+                for half in range(2):
+                    nc.sync.dma_start(
+                        out=out[1 + 2 * pair + half, b].rearrange("c h w -> c (h w)"),
+                        in_=result_tiles[pair][half * HID : (half + 1) * HID, :],
+                    )
+
+        for k, (b, wt) in enumerate(pixel_tiles):
+            regroup(b, wt)
+            if k + 1 < len(attention_sets):
+                write_attention_pairs(nc.scalar.copy, *attention_sets[k + 1])
+            weigh(UPPER, b, wt, 0)
+            weigh(UPPER, b, wt, 1)
+            weigh(LOWER, b, wt, 0)
+            quantise(UPPER, b, wt)
+            convolve(UPPER, b, wt)
+            weigh(LOWER, b, wt, 1)
+            if k > 0:
+                take_statistics(UPPER, *pixel_tiles[k - 1])
+            quantise(LOWER, b, wt)
+        take_statistics(UPPER, *pixel_tiles[-1])
         half_h0 = keep.tile([P, PIXELS], F32)
         nc.scalar.mul(out=half_h0[:], in_=h0[:], mul=0.5)
+        gain_and_shift(UPPER)
+
         node0 = keep.tile([P, PIXELS], F32)
         nc.vector.scalar_tensor_tensor(
             out=node0[:], in0=p0[:], scalar=0.5, in1=half_h0[:], op0=ALU.mult, op1=ALU.add
         )
         nc.sync.dma_start(out=out[0].rearrange("b c h w -> (b c) (h w)"), in_=node0[:])
 
-        finish(UPPER)
-        for b in range(IMAGES):
-            for wt in range(PIXEL_TILES):
-                convolve(LOWER, b, wt)
-        finish(LOWER)
+        upper_banks = [(pair, b, wt) for (b, wt) in pixel_tiles for pair in PAIRS_OF[UPPER]]
+        for k, (b, wt) in enumerate(pixel_tiles):
+            finish_bank(*upper_banks[k])
+            convolve(LOWER, b, wt)
+            take_statistics(LOWER, b, wt)
+        gain_and_shift(LOWER)
+        for bank in upper_banks[len(pixel_tiles) :]:
+            finish_bank(*bank)
+        for b, wt in pixel_tiles:
+            finish_bank(PAIRS_OF[LOWER][0], b, wt)

@@ -28,6 +28,7 @@ N_PAIRS = 3
 OUT_CHANNELS = N_PAIRS * P
 QUADRANTS = 4
 STATS = 6
+TUPLE = 3
 EPS = 1e-5
 
 FLOPS = 2 * OUT_CHANNELS * CHANNELS * IMAGES * PIXELS
@@ -52,7 +53,7 @@ def tile_gnn_kernel(
         keep = stack.enter_context(tc.tile_pool(name="keep", bufs=1))
         products = stack.enter_context(tc.tile_pool(name="products", bufs=3))
         quantised = stack.enter_context(tc.tile_pool(name="quantised", bufs=1))
-        results = stack.enter_context(tc.tile_pool(name="results", bufs=3))
+        results = stack.enter_context(tc.tile_pool(name="results", bufs=4))
         psum = stack.enter_context(tc.psum_pool(name="psum", bufs=8))
 
         att_row = keep.tile([P, 2, IMAGES, PIXELS], BF16)
@@ -76,7 +77,7 @@ def tile_gnn_kernel(
         nc.scalar.dma_start(out=affine_rows[3:5, :], in_=beta_u.rearrange("(r c) -> r c", c=P))
         nc.scalar.dma_start(out=affine_rows[5:6, :], in_=beta_l.rearrange("(r c) -> r c", c=P))
         table_warmer = keep.tile([P, 1], F32)
-        nc.scalar.activation(out=table_warmer[:], in_=eps[:], func=ACT.Sqrt)
+        nc.scalar.activation(out=table_warmer[:], in_=eps[:], func=ACT.Abs_reciprocal_sqrt)
         for scales, first, width in ((Wu_scales, 0, 2 * P), (Wl_scales, 2 * P, P)):
             for quadrant in range(QUADRANTS):
                 nc.gpsimd.dma_start(
@@ -154,8 +155,8 @@ def tile_gnn_kernel(
 
         affine_ps = psum.tile([P, P], BF16, tag="bank")
         nc.tensor.transpose(out=affine_ps[:], in_=affine_rows[:], identity=identity[:])
-        affine = keep.tile([P, 2 * N_PAIRS], F32)
-        nc.vector.tensor_copy(out=affine[:], in_=affine_ps[:, 0 : 2 * N_PAIRS])
+        half_affine = keep.tile([P, 2 * N_PAIRS], F32)
+        nc.vector.tensor_scalar_mul(out=half_affine[:], in0=affine_ps[:, 0 : 2 * N_PAIRS], scalar1=0.5)
 
         spread_attention(*attention_sets[2])
         spread_attention(*attention_sets[3])
@@ -163,13 +164,12 @@ def tile_gnn_kernel(
         pixel_tiles = [(b, wt) for b in range(IMAGES) for wt in range(PIXEL_TILES)]
         xp_grouped = keep.tile([P, IMAGES, PASSES, PIXELS, PACK], BF16)
 
-        def regroup(b, wt):
+        def regroup(copy, b, wt, g):
             cols = slice(wt * N_TILE, (wt + 1) * N_TILE)
-            for g in range(PASSES):
-                nc.scalar.copy(
-                    out=xp_grouped[:, b, g, cols, :].rearrange("p (c i) t -> p c t i", i=4),
-                    in_=xp_rows[:, b, g, :, cols].rearrange("p t (c i) -> p c t i", i=4),
-                )
+            copy(
+                out=xp_grouped[:, b, g, cols, :].rearrange("p (c i) t -> p c t i", i=4),
+                in_=xp_rows[:, b, g, :, cols].rearrange("p t (c i) -> p c t i", i=4),
+            )
 
         weighted_tiles = {}
 
@@ -220,79 +220,111 @@ def tile_gnn_kernel(
                     )
                 y_banks[(pair, b, wt)] = y
 
-        stats = keep.tile([P, N_PAIRS, len(pixel_tiles), STATS], F32)
+        scalar_tiles = {UPPER: len(pixel_tiles) - 1, LOWER: 0}
+        stats = keep.tile([P, N_PAIRS, len(pixel_tiles) * STATS], F32)
+        scalar_stats = keep.tile([P, len(PAIRS_OF[UPPER]), scalar_tiles[UPPER], 2], F32)
+        nc.vector.memset(stats[:, 0 : len(PAIRS_OF[UPPER]), 0 : scalar_tiles[UPPER] * TUPLE], float(N_TILE))
 
-        def take_statistics(product, b, wt):
+        def scalar_statistics(k):
+            b, wt = pixel_tiles[k]
+            for pair in PAIRS_OF[UPPER]:
+                unused = results.tile([P, N_TILE], BF16)
+                nc.scalar.activation(
+                    out=unused[:], in_=y_banks[(pair, b, wt)][:], func=ACT.Copy, scale=1.0 / N_TILE,
+                    accum_out=scalar_stats[:, pair, k, 0:1],
+                )
+            for pair in PAIRS_OF[UPPER]:
+                unused = results.tile([P, N_TILE], BF16)
+                nc.scalar.activation(
+                    out=unused[:], in_=y_banks[(pair, b, wt)][:], func=ACT.Square, scale=-1.0,
+                    bias=scalar_stats[:, pair, k, 0:1], accum_out=scalar_stats[:, pair, k, 1:2],
+                )
+
+        def vector_statistics(product, k):
+            b, wt = pixel_tiles[k]
+            first = scalar_tiles[product] * TUPLE + (k - scalar_tiles[product]) * STATS
             for pair in PAIRS_OF[product]:
-                nc.vector.bn_stats(out=stats[:, pair, b * PIXEL_TILES + wt, :], in_=y_banks[(pair, b, wt)][:])
+                nc.vector.bn_stats(out=stats[:, pair, first : first + STATS], in_=y_banks[(pair, b, wt)][:])
 
         mean_var = keep.tile([P, N_PAIRS, 2], F32)
-        std = keep.tile([P, N_PAIRS], F32)
+        minus_mean_gamma = keep.tile([P, N_PAIRS], F32)
         inv_std = keep.tile([P, N_PAIRS], F32)
         gain = keep.tile([P, N_PAIRS], F32)
-        mean_gain = keep.tile([P, N_PAIRS], F32)
         shift = keep.tile([P, N_PAIRS], F32)
 
         def gain_and_shift(product):
             pairs = PAIRS_OF[product]
             these = slice(pairs[0], pairs[-1] + 1)
+            used = scalar_tiles[product] * TUPLE + (len(pixel_tiles) - scalar_tiles[product]) * STATS
             for pair in pairs:
-                nc.vector.bn_aggr(out=mean_var[:, pair, :], in_=stats[:, pair].rearrange("p u s -> p (u s)"))
-            nc.scalar.activation(out=std[:, these], in_=mean_var[:, these, 1], func=ACT.Sqrt, bias=eps[:])
-            nc.vector.reciprocal(out=inv_std[:, these], in_=std[:, these])
+                nc.vector.bn_aggr(out=mean_var[:, pair, :], in_=stats[:, pair, 0:used])
             nc.vector.scalar_tensor_tensor(
-                out=gain[:, these], in0=affine[:, these], scalar=0.5, in1=inv_std[:, these],
+                out=minus_mean_gamma[:, these], in0=mean_var[:, these, 0], scalar=-1.0, in1=half_affine[:, these],
                 op0=ALU.mult, op1=ALU.mult,
             )
-            nc.vector.tensor_tensor(
-                out=mean_gain[:, these], in0=mean_var[:, these, 0], in1=gain[:, these], op=ALU.mult
+            nc.scalar.activation(
+                out=inv_std[:, these], in_=mean_var[:, these, 1], func=ACT.Abs_reciprocal_sqrt, bias=eps[:]
             )
-            nc.vector.scalar_tensor_tensor(
-                out=shift[:, these], in0=affine[:, N_PAIRS + pairs[0] : N_PAIRS + pairs[-1] + 1], scalar=0.5,
-                in1=mean_gain[:, these], op0=ALU.mult, op1=ALU.subtract,
-            )
+            for pair in pairs:
+                one = slice(pair, pair + 1)
+                nc.scalar.activation(out=gain[:, one], in_=half_affine[:, one], func=ACT.Copy, scale=inv_std[:, one])
+                nc.scalar.activation(
+                    out=shift[:, one], in_=minus_mean_gamma[:, one], func=ACT.Identity, scale=inv_std[:, one],
+                    bias=half_affine[:, N_PAIRS + pair : N_PAIRS + pair + 1],
+                )
 
-        result_tiles = {}
+        half_relus = {}
 
-        def finish_bank(pair, b, wt):
-            if wt == 0:
-                result = results.tile([P, PIXELS], F32)
-                result_tiles[pair] = result
-            cols = slice(wt * N_TILE, (wt + 1) * N_TILE)
-            half_relu = results.tile([P, N_TILE], F32)
+        def normalise(pair, b, wt):
+            half_relu = results.tile([P, N_TILE], F32, bufs=6)
             nc.scalar.activation(
                 out=half_relu[:], in_=y_banks[(pair, b, wt)][:], func=ACT.Relu,
                 bias=shift[:, pair : pair + 1], scale=gain[:, pair : pair + 1],
             )
+            half_relus[(pair, b, wt)] = half_relu
+
+        def add_node(pair, b, wt):
+            cols = slice(wt * N_TILE, (wt + 1) * N_TILE)
+            result = results.tile([P, N_TILE], F32)
             nc.vector.scalar_tensor_tensor(
-                out=result_tiles[pair][:, cols], in0=p_pairs[:, pair, b, cols], scalar=0.5, in1=half_relu[:],
+                out=result[:], in0=p_pairs[:, pair, b, cols], scalar=0.5, in1=half_relus[(pair, b, wt)][:],
                 op0=ALU.mult, op1=ALU.add,
             )
-            if wt == PIXEL_TILES - 1:
-                for half in range(2):
-                    nc.sync.dma_start(
-                        out=out[1 + 2 * pair + half, b].rearrange("c h w -> c (h w)"),
-                        in_=result_tiles[pair][half * HID : (half + 1) * HID, :],
-                    )
+            for half in range(2):
+                nc.sync.dma_start(
+                    out=out[1 + 2 * pair + half, b].rearrange("c h w -> c (h w)")[:, cols],
+                    in_=result[half * HID : (half + 1) * HID, :],
+                )
 
+        last = len(pixel_tiles) - 1
         for k, (b, wt) in enumerate(pixel_tiles):
-            regroup(b, wt)
+            regroup(nc.scalar.copy, b, wt, 0)
+            regroup(nc.vector.tensor_copy if k == 0 else nc.scalar.copy, b, wt, 1)
             if k + 1 < len(attention_sets):
                 write_attention_pairs(nc.scalar.copy, *attention_sets[k + 1])
+            if k >= 2:
+                scalar_statistics(k - 2)
             weigh(UPPER, b, wt, 0)
+            if k > 0:
+                quantise(LOWER, *pixel_tiles[k - 1])
             weigh(UPPER, b, wt, 1)
             weigh(LOWER, b, wt, 0)
             quantise(UPPER, b, wt)
             convolve(UPPER, b, wt)
             weigh(LOWER, b, wt, 1)
-            if k > 0:
-                take_statistics(UPPER, *pixel_tiles[k - 1])
-            quantise(LOWER, b, wt)
-        take_statistics(UPPER, *pixel_tiles[-1])
-        half_h0 = keep.tile([P, PIXELS], F32)
-        nc.scalar.mul(out=half_h0[:], in_=h0[:], mul=0.5)
-        gain_and_shift(UPPER)
+        scalar_statistics(last - 1)
 
+        half_h0 = keep.tile([P, PIXELS], BF16)
+        nc.vector.tensor_scalar_mul(out=half_h0[:], in0=h0[:], scalar1=0.5)
+        vector_statistics(UPPER, last)
+        nc.vector.tensor_copy(
+            out=stats[:, 0 : len(PAIRS_OF[UPPER]), 0 : scalar_tiles[UPPER] * TUPLE].rearrange(
+                "p r (k s) -> p r k s", s=TUPLE
+            )[:, :, :, 1:TUPLE],
+            in_=scalar_stats[:],
+        )
+        gain_and_shift(UPPER)
+        quantise(LOWER, *pixel_tiles[last])
         node0 = keep.tile([P, PIXELS], F32)
         nc.vector.scalar_tensor_tensor(
             out=node0[:], in0=p0[:], scalar=0.5, in1=half_h0[:], op0=ALU.mult, op1=ALU.add
@@ -300,12 +332,19 @@ def tile_gnn_kernel(
         nc.sync.dma_start(out=out[0].rearrange("b c h w -> (b c) (h w)"), in_=node0[:])
 
         upper_banks = [(pair, b, wt) for (b, wt) in pixel_tiles for pair in PAIRS_OF[UPPER]]
+        lower_banks = [(PAIRS_OF[LOWER][0], b, wt) for (b, wt) in pixel_tiles]
         for k, (b, wt) in enumerate(pixel_tiles):
-            finish_bank(*upper_banks[k])
+            normalise(*upper_banks[k])
+            add_node(*upper_banks[k])
             convolve(LOWER, b, wt)
-            take_statistics(LOWER, b, wt)
+            if k > 0:
+                vector_statistics(LOWER, k - 1)
+        vector_statistics(LOWER, last)
+        for bank in upper_banks[len(pixel_tiles) :]:
+            normalise(*bank)
         gain_and_shift(LOWER)
         for bank in upper_banks[len(pixel_tiles) :]:
-            finish_bank(*bank)
-        for b, wt in pixel_tiles:
-            finish_bank(PAIRS_OF[LOWER][0], b, wt)
+            add_node(*bank)
+        for bank in lower_banks:
+            normalise(*bank)
+            add_node(*bank)

@@ -225,7 +225,7 @@ def tile_gnn_kernel(
         scalar_stats = keep.tile([P, len(PAIRS_OF[UPPER]), scalar_tiles[UPPER], 2], F32)
         nc.vector.memset(stats[:, 0 : len(PAIRS_OF[UPPER]), 0 : scalar_tiles[UPPER] * TUPLE], float(N_TILE))
 
-        def scalar_statistics(k):
+        def scalar_means(k):
             b, wt = pixel_tiles[k]
             for pair in PAIRS_OF[UPPER]:
                 unused = results.tile([P, N_TILE], BF16)
@@ -233,6 +233,9 @@ def tile_gnn_kernel(
                     out=unused[:], in_=y_banks[(pair, b, wt)][:], func=ACT.Copy, scale=1.0 / N_TILE,
                     accum_out=scalar_stats[:, pair, k, 0:1],
                 )
+
+        def scalar_squares(k):
+            b, wt = pixel_tiles[k]
             for pair in PAIRS_OF[UPPER]:
                 unused = results.tile([P, N_TILE], BF16)
                 nc.scalar.activation(
@@ -302,8 +305,6 @@ def tile_gnn_kernel(
             regroup(nc.vector.tensor_copy if k == 0 else nc.scalar.copy, b, wt, 1)
             if k + 1 < len(attention_sets):
                 write_attention_pairs(nc.scalar.copy, *attention_sets[k + 1])
-            if k >= 2:
-                scalar_statistics(k - 2)
             weigh(UPPER, b, wt, 0)
             if k > 0:
                 quantise(LOWER, *pixel_tiles[k - 1])
@@ -312,7 +313,10 @@ def tile_gnn_kernel(
             quantise(UPPER, b, wt)
             convolve(UPPER, b, wt)
             weigh(LOWER, b, wt, 1)
-        scalar_statistics(last - 1)
+        for k in range(scalar_tiles[UPPER]):
+            scalar_means(k)
+        for k in range(scalar_tiles[UPPER]):
+            scalar_squares(k)
 
         half_h0 = keep.tile([P, PIXELS], BF16)
         nc.vector.tensor_scalar_mul(out=half_h0[:], in0=h0[:], scalar1=0.5)

@@ -30,6 +30,10 @@ QUADRANTS = 4
 STATS = 6
 TUPLE = 3
 EPS = 1e-5
+CHUNKS = PIXELS // P
+SCALAR_TILES = 3
+Y_BANKS = 6
+ATT_BANKS = 2
 
 FLOPS = 2 * OUT_CHANNELS * CHANNELS * IMAGES * PIXELS
 BYTES = (
@@ -52,25 +56,25 @@ def tile_gnn_kernel(
         stack.enter_context(tc.manual_schedule())
         keep = stack.enter_context(tc.tile_pool(name="keep", bufs=1))
         products = stack.enter_context(tc.tile_pool(name="products", bufs=3))
-        quantised = stack.enter_context(tc.tile_pool(name="quantised", bufs=1))
+        quantised = stack.enter_context(tc.tile_pool(name="quantised", bufs=4))
         results = stack.enter_context(tc.tile_pool(name="results", bufs=4))
-        psum = stack.enter_context(tc.psum_pool(name="psum", bufs=8))
+        psum = stack.enter_context(tc.psum_pool(name="psum", bufs=1))
 
-        att_row = keep.tile([P, 2, IMAGES, PIXELS], BF16)
+        pixel_tiles = [(b, wt) for b in range(IMAGES) for wt in range(PIXEL_TILES)]
+        last = len(pixel_tiles) - 1
+
+        att_rows = keep.tile([P, P], BF16)
         affine_rows = keep.tile([P, P], BF16)
         w_scales = keep.tile([P, PASSES, OUT_CHANNELS], U8, align_bytes=64)
         eps = keep.tile([P, 1], F32)
-        ones = keep.tile([P, P], BF16)
-        nc.vector.memset(att_row[:, UPPER, 0].bitcast(I32), 0)
+        nc.vector.memset(att_rows[:].bitcast(I32), 0)
         nc.vector.memset(eps[:], EPS)
         nc.vector.memset(affine_rows[:].bitcast(I32), 0)
         nc.vector.memset(w_scales[:].rearrange("p g n -> p (g n)").bitcast(I32), 0)
-        nc.vector.memset(ones[:], 1.0)
-        nc.vector.memset(att_row[:, LOWER, 0].bitcast(I32), 0)
-        nc.vector.memset(att_row[:, UPPER, 1].bitcast(I32), 0)
-        nc.vector.memset(att_row[:, LOWER, 1].bitcast(I32), 0)
         identity = keep.tile([P, P], BF16)
         make_identity(nc, identity[:])
+        identity_words = keep.tile([P, P], F32)
+        make_identity(nc, identity_words[:])
 
         nc.scalar.dma_start(out=affine_rows[0:2, :], in_=gamma_u.rearrange("(r c) -> r c", c=P))
         nc.scalar.dma_start(out=affine_rows[2:3, :], in_=gamma_l.rearrange("(r c) -> r c", c=P))
@@ -88,9 +92,6 @@ def tile_gnn_kernel(
         xp_rows = keep.tile([P, IMAGES, PASSES, PACK, PIXELS], BF16)
         w_words = keep.tile([P, PASSES, OUT_CHANNELS], U32, align_bytes=64)
 
-        def load_attention(product, b):
-            nc.sync.dma_start(out=att_row[0:1, product, b], in_=h_att[1 + product, b].rearrange("o h w -> o (h w)"))
-
         def load_pixels(b, wt):
             for g in range(PASSES):
                 nc.sync.dma_start(
@@ -100,11 +101,11 @@ def tile_gnn_kernel(
                     ],
                 )
 
-        load_attention(UPPER, 0)
+        nc.sync.dma_start(
+            out=att_rows[0 : 2 * IMAGES * CHUNKS, :],
+            in_=h_att[1:3].rearrange("a b o (c h) w -> (a b o c) (h w)", c=CHUNKS),
+        )
         load_pixels(0, 0)
-        load_attention(LOWER, 0)
-        load_attention(UPPER, 1)
-        load_attention(LOWER, 1)
         load_pixels(0, 1)
         nc.sync.dma_start(
             out=w_words[:, :, 0 : 2 * P].bitcast(I32),
@@ -128,43 +129,40 @@ def tile_gnn_kernel(
                     in_=p_nodes[1 + 2 * pair + half].rearrange("b c h w -> c b (h w)"),
                 )
 
-        attention_sets = [(product, b) for b in range(IMAGES) for product in (UPPER, LOWER)]
+        att_cols_ps = psum.tile([P, P], BF16, tag="y", bufs=Y_BANKS)
+        nc.tensor.transpose(out=att_cols_ps[:], in_=att_rows[:], identity=identity[:])
+        att_words = keep.tile([P, 2 * IMAGES * CHUNKS, 2], BF16)
+        nc.vector.tensor_copy(
+            out=att_words[:],
+            in_=att_cols_ps[:, 0 : 2 * IMAGES * CHUNKS].unsqueeze(2).to_broadcast([P, 2 * IMAGES * CHUNKS, 2]),
+        )
         att_banks = {}
 
-        def spread_attention(product, b):
-            for wt in range(PIXEL_TILES):
-                att_ps = psum.tile([P, N_TILE], F32, tag="bank")
-                nc.tensor.matmul(
-                    out=att_ps[:], lhsT=ones[:], rhs=att_row[:, product, b, wt * N_TILE : (wt + 1) * N_TILE],
-                    start=True, stop=True,
+        def spread_attention(product, k):
+            b, wt = pixel_tiles[k]
+            att_ps = psum.tile([P, N_TILE], F32, tag="att", bufs=ATT_BANKS)
+            for c in range(N_TILE // P):
+                j = (product * IMAGES + b) * CHUNKS + wt * (N_TILE // P) + c
+                nc.tensor.transpose(
+                    out=att_ps[:, c * P : (c + 1) * P],
+                    in_=att_words[:].rearrange("p j e -> p (j e)").bitcast(F32)[:, j : j + 1].to_broadcast([P, P]),
+                    identity=identity_words[:],
                 )
-                att_banks[(product, b, wt)] = att_ps
+            att_banks[(product, k)] = att_ps
 
-        att_pairs = keep.tile([P, 2, IMAGES, PIXELS, 2], BF16)
+        units = [(UPPER, 0), (LOWER, 0), (UPPER, 1), (LOWER, 1), (UPPER, 2), (UPPER, 3), (LOWER, 2), (LOWER, 3)]
+        spread_attention(*units[0])
+        spread_attention(*units[1])
 
-        def write_attention_pairs(copy, product, b):
-            for wt in range(PIXEL_TILES):
-                copy(
-                    out=att_pairs[:, product, b, wt * N_TILE : (wt + 1) * N_TILE, :],
-                    in_=att_banks[(product, b, wt)][:].unsqueeze(2).to_broadcast([P, N_TILE, 2]),
-                )
-
-        spread_attention(*attention_sets[0])
-        spread_attention(*attention_sets[1])
-        write_attention_pairs(nc.vector.tensor_copy, *attention_sets[0])
-
-        affine_ps = psum.tile([P, P], BF16, tag="bank")
+        affine_ps = psum.tile([P, P], BF16, tag="y", bufs=Y_BANKS)
         nc.tensor.transpose(out=affine_ps[:], in_=affine_rows[:], identity=identity[:])
         half_affine = keep.tile([P, 2 * N_PAIRS], F32)
-        nc.vector.tensor_scalar_mul(out=half_affine[:], in0=affine_ps[:, 0 : 2 * N_PAIRS], scalar1=0.5)
+        kept_gamma = keep.tile([P, N_PAIRS], F32)
 
-        spread_attention(*attention_sets[2])
-        spread_attention(*attention_sets[3])
-
-        pixel_tiles = [(b, wt) for b in range(IMAGES) for wt in range(PIXEL_TILES)]
         xp_grouped = keep.tile([P, IMAGES, PASSES, PIXELS, PACK], BF16)
 
-        def regroup(copy, b, wt, g):
+        def regroup(copy, k, g):
+            b, wt = pixel_tiles[k]
             cols = slice(wt * N_TILE, (wt + 1) * N_TILE)
             copy(
                 out=xp_grouped[:, b, g, cols, :].rearrange("p (c i) t -> p c t i", i=4),
@@ -173,41 +171,32 @@ def tile_gnn_kernel(
 
         weighted_tiles = {}
 
-        def weigh(product, b, wt, g):
-            if g == 0:
+        def weigh(product, k, g):
+            b, wt = pixel_tiles[k]
+            if (product, k) not in weighted_tiles:
                 weighted = products.tile([P, PASSES, N_TILE, PACK], BF16, align_bytes=64)
-                weighted_tiles[product] = weighted
+                weighted_tiles[(product, k)] = weighted
             cols = slice(wt * N_TILE, (wt + 1) * N_TILE)
             nc.vector.tensor_tensor(
-                out=weighted_tiles[product][:, g].rearrange("p w (u e) -> p w u e", e=2),
+                out=weighted_tiles[(product, k)][:, g].rearrange("p w (u e) -> p w u e", e=2),
                 in0=xp_grouped[:, b, g, cols, :].rearrange("p w (u e) -> p w u e", e=2),
-                in1=att_pairs[:, product, b, cols, :].unsqueeze(2).to_broadcast([P, N_TILE, 2, 2]),
+                in1=att_banks[(product, k)][:].bitcast(BF16).rearrange("p (w e) -> p w e", e=2)
+                .unsqueeze(2).to_broadcast([P, N_TILE, 2, 2]),
                 op=ALU.mult,
             )
 
-        quantised_tiles = {}
-        places = {UPPER: 2, LOWER: len(pixel_tiles)}
+        y_banks = {}
 
-        def quantise(product, b, wt):
-            codes = quantised.tile(
-                [P, PASSES * N_TILE], U32, align_bytes=64, tag="codes%d" % product, bufs=places[product]
-            )
-            scales = quantised.tile(
-                [P, PASSES * N_TILE], U8, align_bytes=64, tag="scales%d" % product, bufs=places[product]
-            )
+        def quantise_and_convolve(product, k):
+            codes = quantised.tile([P, PASSES * N_TILE], U32, align_bytes=64)
+            scales = quantised.tile([P, PASSES * N_TILE], U8, align_bytes=64)
             nc.vector.quantize_mx(
                 out=codes[:].bitcast(FP8X4),
                 scales=scales[:],
-                in_=weighted_tiles[product][:].rearrange("p g w t -> p (g w t)"),
+                in_=weighted_tiles[(product, k)][:].rearrange("p g w t -> p (g w t)"),
             )
-            quantised_tiles[(product, b, wt)] = (codes, scales)
-
-        y_banks = {}
-
-        def convolve(product, b, wt):
-            codes, scales = quantised_tiles[(product, b, wt)]
             for pair in PAIRS_OF[product]:
-                y = psum.tile([P, N_TILE], F32, tag="bank")
+                y = psum.tile([P, N_TILE], F32, tag="y", bufs=Y_BANKS)
                 for g in range(PASSES):
                     nc.tensor.matmul_mx(
                         out=y[:],
@@ -218,79 +207,88 @@ def tile_gnn_kernel(
                         start=(g == 0),
                         stop=(g == PASSES - 1),
                     )
-                y_banks[(pair, b, wt)] = y
+                y_banks[(pair, k)] = y
 
-        scalar_tiles = {UPPER: len(pixel_tiles) - 1, LOWER: 0}
-        stats = keep.tile([P, N_PAIRS, len(pixel_tiles) * STATS], F32)
-        scalar_stats = keep.tile([P, len(PAIRS_OF[UPPER]), scalar_tiles[UPPER], 2], F32)
-        nc.vector.memset(stats[:, 0 : len(PAIRS_OF[UPPER]), 0 : scalar_tiles[UPPER] * TUPLE], float(N_TILE))
+        stats = keep.tile([P, N_PAIRS, SCALAR_TILES * TUPLE + (len(pixel_tiles) - SCALAR_TILES) * STATS], F32)
+        y_kept = keep.tile([P, N_PAIRS, SCALAR_TILES, N_TILE], F32)
 
-        def scalar_means(k):
-            b, wt = pixel_tiles[k]
-            for pair in PAIRS_OF[UPPER]:
-                unused = results.tile([P, N_TILE], BF16)
+        def scalar_statistics(product, k):
+            for pair in PAIRS_OF[product]:
                 nc.scalar.activation(
-                    out=unused[:], in_=y_banks[(pair, b, wt)][:], func=ACT.Copy, scale=1.0 / N_TILE,
-                    accum_out=scalar_stats[:, pair, k, 0:1],
+                    out=y_kept[:, pair, k, :], in_=y_banks[(pair, k)][:], func=ACT.Copy, scale=1.0 / N_TILE,
+                    accum_out=stats[:, pair, k * TUPLE + 1 : k * TUPLE + 2],
                 )
-
-        def scalar_squares(k):
-            b, wt = pixel_tiles[k]
-            for pair in PAIRS_OF[UPPER]:
+            for pair in PAIRS_OF[product]:
                 unused = results.tile([P, N_TILE], BF16)
                 nc.scalar.activation(
-                    out=unused[:], in_=y_banks[(pair, b, wt)][:], func=ACT.Square, scale=-1.0,
-                    bias=scalar_stats[:, pair, k, 0:1], accum_out=scalar_stats[:, pair, k, 1:2],
+                    out=unused[:], in_=y_kept[:, pair, k, :], func=ACT.Square, scale=-float(N_TILE),
+                    bias=stats[:, pair, k * TUPLE + 1 : k * TUPLE + 2],
+                    accum_out=stats[:, pair, k * TUPLE + 2 : k * TUPLE + 3],
                 )
 
         def vector_statistics(product, k):
-            b, wt = pixel_tiles[k]
-            first = scalar_tiles[product] * TUPLE + (k - scalar_tiles[product]) * STATS
+            first = SCALAR_TILES * TUPLE + (k - SCALAR_TILES) * STATS
             for pair in PAIRS_OF[product]:
-                nc.vector.bn_stats(out=stats[:, pair, first : first + STATS], in_=y_banks[(pair, b, wt)][:])
+                nc.vector.bn_stats(out=stats[:, pair, first : first + STATS], in_=y_banks[(pair, k)][:])
 
         mean_var = keep.tile([P, N_PAIRS, 2], F32)
         minus_mean_gamma = keep.tile([P, N_PAIRS], F32)
         inv_std = keep.tile([P, N_PAIRS], F32)
         gain = keep.tile([P, N_PAIRS], F32)
+        kept_gain = keep.tile([P, N_PAIRS], F32)
         shift = keep.tile([P, N_PAIRS], F32)
 
-        def gain_and_shift(product):
+        def mean_and_variance(product):
             pairs = PAIRS_OF[product]
             these = slice(pairs[0], pairs[-1] + 1)
-            used = scalar_tiles[product] * TUPLE + (len(pixel_tiles) - scalar_tiles[product]) * STATS
             for pair in pairs:
-                nc.vector.bn_aggr(out=mean_var[:, pair, :], in_=stats[:, pair, 0:used])
+                nc.vector.bn_aggr(out=mean_var[:, pair, :], in_=stats[:, pair, :])
             nc.vector.scalar_tensor_tensor(
                 out=minus_mean_gamma[:, these], in0=mean_var[:, these, 0], scalar=-1.0, in1=half_affine[:, these],
                 op0=ALU.mult, op1=ALU.mult,
             )
+
+        def gain_and_shift(product):
+            pairs = PAIRS_OF[product]
+            these = slice(pairs[0], pairs[-1] + 1)
             nc.scalar.activation(
                 out=inv_std[:, these], in_=mean_var[:, these, 1], func=ACT.Abs_reciprocal_sqrt, bias=eps[:]
             )
             for pair in pairs:
                 one = slice(pair, pair + 1)
-                nc.scalar.activation(out=gain[:, one], in_=half_affine[:, one], func=ACT.Copy, scale=inv_std[:, one])
+                nc.scalar.activation(out=kept_gain[:, one], in_=kept_gamma[:, one], func=ACT.Copy, scale=inv_std[:, one])
                 nc.scalar.activation(
                     out=shift[:, one], in_=minus_mean_gamma[:, one], func=ACT.Identity, scale=inv_std[:, one],
                     bias=half_affine[:, N_PAIRS + pair : N_PAIRS + pair + 1],
                 )
 
+        def plain_gain(product):
+            for pair in PAIRS_OF[product]:
+                one = slice(pair, pair + 1)
+                nc.scalar.activation(out=gain[:, one], in_=half_affine[:, one], func=ACT.Copy, scale=inv_std[:, one])
+
         half_relus = {}
 
-        def normalise(pair, b, wt):
+        def normalise(pair, k):
             half_relu = results.tile([P, N_TILE], F32, bufs=6)
-            nc.scalar.activation(
-                out=half_relu[:], in_=y_banks[(pair, b, wt)][:], func=ACT.Relu,
-                bias=shift[:, pair : pair + 1], scale=gain[:, pair : pair + 1],
-            )
-            half_relus[(pair, b, wt)] = half_relu
+            if k < SCALAR_TILES:
+                nc.scalar.activation(
+                    out=half_relu[:], in_=y_kept[:, pair, k, :], func=ACT.Relu,
+                    bias=shift[:, pair : pair + 1], scale=kept_gain[:, pair : pair + 1],
+                )
+            else:
+                nc.scalar.activation(
+                    out=half_relu[:], in_=y_banks[(pair, k)][:], func=ACT.Relu,
+                    bias=shift[:, pair : pair + 1], scale=gain[:, pair : pair + 1],
+                )
+            half_relus[(pair, k)] = half_relu
 
-        def add_node(pair, b, wt):
+        def add_node(pair, k):
+            b, wt = pixel_tiles[k]
             cols = slice(wt * N_TILE, (wt + 1) * N_TILE)
             result = results.tile([P, N_TILE], F32)
             nc.vector.scalar_tensor_tensor(
-                out=result[:], in0=p_pairs[:, pair, b, cols], scalar=0.5, in1=half_relus[(pair, b, wt)][:],
+                out=result[:], in0=p_pairs[:, pair, b, cols], scalar=0.5, in1=half_relus[(pair, k)][:],
                 op0=ALU.mult, op1=ALU.add,
             )
             for half in range(2):
@@ -299,56 +297,67 @@ def tile_gnn_kernel(
                     in_=result[half * HID : (half + 1) * HID, :],
                 )
 
-        last = len(pixel_tiles) - 1
-        for k, (b, wt) in enumerate(pixel_tiles):
-            regroup(nc.scalar.copy, b, wt, 0)
-            regroup(nc.vector.tensor_copy if k == 0 else nc.scalar.copy, b, wt, 1)
-            if k + 1 < len(attention_sets):
-                write_attention_pairs(nc.scalar.copy, *attention_sets[k + 1])
-            weigh(UPPER, b, wt, 0)
-            if k > 0:
-                quantise(LOWER, *pixel_tiles[k - 1])
-            weigh(UPPER, b, wt, 1)
-            weigh(LOWER, b, wt, 0)
-            quantise(UPPER, b, wt)
-            convolve(UPPER, b, wt)
-            weigh(LOWER, b, wt, 1)
-        for k in range(scalar_tiles[UPPER]):
-            scalar_means(k)
-        for k in range(scalar_tiles[UPPER]):
-            scalar_squares(k)
+        regroup(nc.vector.tensor_copy, 0, 0)
+        regroup(nc.scalar.copy, 0, 1)
+        for k in range(1, len(pixel_tiles)):
+            regroup(nc.scalar.copy, k, 0)
+            regroup(nc.scalar.copy, k, 1)
+
+        weigh(UPPER, 0, 0)
+        weigh(LOWER, 0, 0)
+        nc.vector.tensor_scalar_mul(out=half_affine[:], in0=affine_ps[:, 0 : 2 * N_PAIRS], scalar1=0.5)
+        nc.vector.tensor_scalar_mul(out=kept_gamma[:], in0=affine_ps[:, 0:N_PAIRS], scalar1=0.5 * N_TILE)
+        nc.vector.memset(stats[:, :, 0 : SCALAR_TILES * TUPLE], float(N_TILE))
+        weigh(UPPER, 0, 1)
+        spread_attention(*units[2])
+        weigh(LOWER, 0, 1)
+        spread_attention(*units[3])
+        quantise_and_convolve(*units[0])
+        for n in range(2, len(units)):
+            weigh(units[n][0], units[n][1], 0)
+            quantise_and_convolve(*units[n - 1])
+            if n == 4:
+                scalar_statistics(UPPER, 0)
+            if n == 5:
+                scalar_statistics(UPPER, 1)
+            if n == 6:
+                scalar_statistics(UPPER, 2)
+                scalar_statistics(LOWER, 0)
+            if n == 7:
+                scalar_statistics(LOWER, 1)
+                vector_statistics(UPPER, last)
+            weigh(units[n][0], units[n][1], 1)
+            if n + 2 < len(units):
+                spread_attention(*units[n + 2])
+        mean_and_variance(UPPER)
+        gain_and_shift(UPPER)
+        quantise_and_convolve(*units[-1])
 
         half_h0 = keep.tile([P, PIXELS], BF16)
         nc.vector.tensor_scalar_mul(out=half_h0[:], in0=h0[:], scalar1=0.5)
-        vector_statistics(UPPER, last)
-        nc.vector.tensor_copy(
-            out=stats[:, 0 : len(PAIRS_OF[UPPER]), 0 : scalar_tiles[UPPER] * TUPLE].rearrange(
-                "p r (k s) -> p r k s", s=TUPLE
-            )[:, :, :, 1:TUPLE],
-            in_=scalar_stats[:],
-        )
-        gain_and_shift(UPPER)
-        quantise(LOWER, *pixel_tiles[last])
         node0 = keep.tile([P, PIXELS], F32)
         nc.vector.scalar_tensor_tensor(
             out=node0[:], in0=p0[:], scalar=0.5, in1=half_h0[:], op0=ALU.mult, op1=ALU.add
         )
         nc.sync.dma_start(out=out[0].rearrange("b c h w -> (b c) (h w)"), in_=node0[:])
 
-        upper_banks = [(pair, b, wt) for (b, wt) in pixel_tiles for pair in PAIRS_OF[UPPER]]
-        lower_banks = [(PAIRS_OF[LOWER][0], b, wt) for (b, wt) in pixel_tiles]
-        for k, (b, wt) in enumerate(pixel_tiles):
-            normalise(*upper_banks[k])
-            add_node(*upper_banks[k])
-            convolve(LOWER, b, wt)
-            if k > 0:
-                vector_statistics(LOWER, k - 1)
+        upper_banks = [(pair, k) for k in range(len(pixel_tiles)) for pair in PAIRS_OF[UPPER]]
+        lower_banks = [(PAIRS_OF[LOWER][0], k) for k in range(len(pixel_tiles))]
         vector_statistics(LOWER, last)
-        for bank in upper_banks[len(pixel_tiles) :]:
+        for bank in upper_banks[0:2]:
             normalise(*bank)
-        gain_and_shift(LOWER)
-        for bank in upper_banks[len(pixel_tiles) :]:
             add_node(*bank)
+        scalar_statistics(LOWER, 2)
+        mean_and_variance(LOWER)
+        for bank in upper_banks[2:6]:
+            normalise(*bank)
+            add_node(*bank)
+        plain_gain(UPPER)
+        for bank in upper_banks[6:8]:
+            normalise(*bank)
+            add_node(*bank)
+        gain_and_shift(LOWER)
+        plain_gain(LOWER)
         for bank in lower_banks:
             normalise(*bank)
             add_node(*bank)

@@ -31,7 +31,7 @@ STATS = 6
 TUPLE = 3
 EPS = 1e-5
 CHUNKS = PIXELS // P
-SCALAR_TILES = 3
+SCALAR_TILES = {UPPER: 4, LOWER: 3}
 Y_BANKS = 6
 ATT_BANKS = 2
 
@@ -67,7 +67,8 @@ def tile_gnn_kernel(
         affine_rows = keep.tile([P, P], BF16)
         w_scales = keep.tile([P, PASSES, OUT_CHANNELS], U8, align_bytes=64)
         eps = keep.tile([P, 1], F32)
-        nc.vector.memset(att_rows[:].bitcast(I32), 0)
+        nc.vector.memset(att_rows[32:64, :].bitcast(I32), 0)
+        nc.vector.memset(att_rows[64:128, :].bitcast(I32), 0)
         nc.vector.memset(eps[:], EPS)
         nc.vector.memset(affine_rows[:].bitcast(I32), 0)
         nc.vector.memset(w_scales[:].rearrange("p g n -> p (g n)").bitcast(I32), 0)
@@ -76,6 +77,10 @@ def tile_gnn_kernel(
         identity_words = keep.tile([P, P], F32)
         make_identity(nc, identity_words[:])
 
+        nc.scalar.dma_start(
+            out=att_rows[0 : 2 * IMAGES * CHUNKS, :],
+            in_=h_att[1:3].rearrange("a b o (c h) w -> (a b o c) (h w)", c=CHUNKS),
+        )
         nc.scalar.dma_start(out=affine_rows[0:2, :], in_=gamma_u.rearrange("(r c) -> r c", c=P))
         nc.scalar.dma_start(out=affine_rows[2:3, :], in_=gamma_l.rearrange("(r c) -> r c", c=P))
         nc.scalar.dma_start(out=affine_rows[3:5, :], in_=beta_u.rearrange("(r c) -> r c", c=P))
@@ -101,10 +106,6 @@ def tile_gnn_kernel(
                     ],
                 )
 
-        nc.sync.dma_start(
-            out=att_rows[0 : 2 * IMAGES * CHUNKS, :],
-            in_=h_att[1:3].rearrange("a b o (c h) w -> (a b o c) (h w)", c=CHUNKS),
-        )
         load_pixels(0, 0)
         load_pixels(0, 1)
         nc.sync.dma_start(
@@ -209,8 +210,14 @@ def tile_gnn_kernel(
                     )
                 y_banks[(pair, k)] = y
 
-        stats = keep.tile([P, N_PAIRS, SCALAR_TILES * TUPLE + (len(pixel_tiles) - SCALAR_TILES) * STATS], F32)
-        y_kept = keep.tile([P, N_PAIRS, SCALAR_TILES, N_TILE], F32)
+        stats_used = {
+            product: SCALAR_TILES[product] * TUPLE + (len(pixel_tiles) - SCALAR_TILES[product]) * STATS
+            for product in (UPPER, LOWER)
+        }
+        stats = keep.tile([P, N_PAIRS, max(stats_used.values())], F32)
+        y_kept = keep.tile([P, N_PAIRS, len(pixel_tiles), N_TILE], F32)
+
+        nc.vector.memset(stats[:], float(N_TILE))
 
         def scalar_statistics(product, k):
             for pair in PAIRS_OF[product]:
@@ -227,7 +234,7 @@ def tile_gnn_kernel(
                 )
 
         def vector_statistics(product, k):
-            first = SCALAR_TILES * TUPLE + (k - SCALAR_TILES) * STATS
+            first = SCALAR_TILES[product] * TUPLE + (k - SCALAR_TILES[product]) * STATS
             for pair in PAIRS_OF[product]:
                 nc.vector.bn_stats(out=stats[:, pair, first : first + STATS], in_=y_banks[(pair, k)][:])
 
@@ -242,7 +249,7 @@ def tile_gnn_kernel(
             pairs = PAIRS_OF[product]
             these = slice(pairs[0], pairs[-1] + 1)
             for pair in pairs:
-                nc.vector.bn_aggr(out=mean_var[:, pair, :], in_=stats[:, pair, :])
+                nc.vector.bn_aggr(out=mean_var[:, pair, :], in_=stats[:, pair, 0 : stats_used[product]])
             nc.vector.scalar_tensor_tensor(
                 out=minus_mean_gamma[:, these], in0=mean_var[:, these, 0], scalar=-1.0, in1=half_affine[:, these],
                 op0=ALU.mult, op1=ALU.mult,
@@ -269,45 +276,45 @@ def tile_gnn_kernel(
 
         half_relus = {}
 
-        def normalise(pair, k):
-            half_relu = results.tile([P, N_TILE], F32, bufs=6)
-            if k < SCALAR_TILES:
+        def normalise(pair, k, tiles):
+            half_relu = results.tile([P, 2 * N_TILE], F32)
+            if k < SCALAR_TILES[UPPER if pair in PAIRS_OF[UPPER] else LOWER]:
                 nc.scalar.activation(
-                    out=half_relu[:], in_=y_kept[:, pair, k, :], func=ACT.Relu,
+                    out=half_relu[:, 0 : tiles * N_TILE],
+                    in_=y_kept[:, pair, k : k + tiles, :].rearrange("p k w -> p (k w)"), func=ACT.Relu,
                     bias=shift[:, pair : pair + 1], scale=kept_gain[:, pair : pair + 1],
                 )
             else:
                 nc.scalar.activation(
-                    out=half_relu[:], in_=y_banks[(pair, k)][:], func=ACT.Relu,
+                    out=half_relu[:, 0:N_TILE], in_=y_banks[(pair, k)][:], func=ACT.Relu,
                     bias=shift[:, pair : pair + 1], scale=gain[:, pair : pair + 1],
                 )
             half_relus[(pair, k)] = half_relu
 
-        def add_node(pair, k):
+        def add_node(pair, k, tiles):
             b, wt = pixel_tiles[k]
-            cols = slice(wt * N_TILE, (wt + 1) * N_TILE)
-            result = results.tile([P, N_TILE], F32)
+            cols = slice(wt * N_TILE, (wt + tiles) * N_TILE)
+            result = results.tile([P, 2 * N_TILE], F32)
             nc.vector.scalar_tensor_tensor(
-                out=result[:], in0=p_pairs[:, pair, b, cols], scalar=0.5, in1=half_relus[(pair, k)][:],
-                op0=ALU.mult, op1=ALU.add,
+                out=result[:, 0 : tiles * N_TILE], in0=p_pairs[:, pair, b, cols], scalar=0.5,
+                in1=half_relus[(pair, k)][:, 0 : tiles * N_TILE], op0=ALU.mult, op1=ALU.add,
             )
             for half in range(2):
                 nc.sync.dma_start(
                     out=out[1 + 2 * pair + half, b].rearrange("c h w -> c (h w)")[:, cols],
-                    in_=result[half * HID : (half + 1) * HID, :],
+                    in_=result[half * HID : (half + 1) * HID, 0 : tiles * N_TILE],
                 )
 
         regroup(nc.vector.tensor_copy, 0, 0)
         regroup(nc.scalar.copy, 0, 1)
+        nc.scalar.activation(out=half_affine[:], in_=affine_ps[:, 0 : 2 * N_PAIRS], func=ACT.Copy, scale=0.5)
+        nc.scalar.activation(out=kept_gamma[:], in_=affine_ps[:, 0:N_PAIRS], func=ACT.Copy, scale=0.5 * N_TILE)
         for k in range(1, len(pixel_tiles)):
             regroup(nc.scalar.copy, k, 0)
             regroup(nc.scalar.copy, k, 1)
 
         weigh(UPPER, 0, 0)
         weigh(LOWER, 0, 0)
-        nc.vector.tensor_scalar_mul(out=half_affine[:], in0=affine_ps[:, 0 : 2 * N_PAIRS], scalar1=0.5)
-        nc.vector.tensor_scalar_mul(out=kept_gamma[:], in0=affine_ps[:, 0:N_PAIRS], scalar1=0.5 * N_TILE)
-        nc.vector.memset(stats[:, :, 0 : SCALAR_TILES * TUPLE], float(N_TILE))
         weigh(UPPER, 0, 1)
         spread_attention(*units[2])
         weigh(LOWER, 0, 1)
@@ -324,8 +331,8 @@ def tile_gnn_kernel(
                 scalar_statistics(UPPER, 2)
                 scalar_statistics(LOWER, 0)
             if n == 7:
+                scalar_statistics(UPPER, 3)
                 scalar_statistics(LOWER, 1)
-                vector_statistics(UPPER, last)
             weigh(units[n][0], units[n][1], 1)
             if n + 2 < len(units):
                 spread_attention(*units[n + 2])
@@ -334,30 +341,25 @@ def tile_gnn_kernel(
         quantise_and_convolve(*units[-1])
 
         half_h0 = keep.tile([P, PIXELS], BF16)
-        nc.vector.tensor_scalar_mul(out=half_h0[:], in0=h0[:], scalar1=0.5)
+        nc.gpsimd.tensor_scalar(out=half_h0[:], in0=h0[:], scalar1=0.5, scalar2=0.0, op0=ALU.mult, op1=ALU.add)
         node0 = keep.tile([P, PIXELS], F32)
         nc.vector.scalar_tensor_tensor(
             out=node0[:], in0=p0[:], scalar=0.5, in1=half_h0[:], op0=ALU.mult, op1=ALU.add
         )
         nc.sync.dma_start(out=out[0].rearrange("b c h w -> (b c) (h w)"), in_=node0[:])
 
-        upper_banks = [(pair, k) for k in range(len(pixel_tiles)) for pair in PAIRS_OF[UPPER]]
-        lower_banks = [(PAIRS_OF[LOWER][0], k) for k in range(len(pixel_tiles))]
+        upper_runs = [(pair, k, PIXEL_TILES) for k in range(0, len(pixel_tiles), PIXEL_TILES) for pair in PAIRS_OF[UPPER]]
+        lower_runs = [(PAIRS_OF[LOWER][0], 0, PIXEL_TILES), (PAIRS_OF[LOWER][0], 2, 1), (PAIRS_OF[LOWER][0], 3, 1)]
         vector_statistics(LOWER, last)
-        for bank in upper_banks[0:2]:
-            normalise(*bank)
-            add_node(*bank)
+        normalise(*upper_runs[0])
+        add_node(*upper_runs[0])
         scalar_statistics(LOWER, 2)
         mean_and_variance(LOWER)
-        for bank in upper_banks[2:6]:
-            normalise(*bank)
-            add_node(*bank)
-        plain_gain(UPPER)
-        for bank in upper_banks[6:8]:
-            normalise(*bank)
-            add_node(*bank)
+        for run in upper_runs[1:]:
+            normalise(*run)
+            add_node(*run)
         gain_and_shift(LOWER)
         plain_gain(LOWER)
-        for bank in lower_banks:
-            normalise(*bank)
-            add_node(*bank)
+        for run in lower_runs:
+            normalise(*run)
+            add_node(*run)

@@ -81,18 +81,8 @@ def tile_gnn_kernel(
             out=att_rows[0 : 2 * IMAGES * CHUNKS, :],
             in_=h_att[1:3].rearrange("a b o (c h) w -> (a b o c) (h w)", c=CHUNKS),
         )
-        nc.scalar.dma_start(out=affine_rows[0:2, :], in_=gamma_u.rearrange("(r c) -> r c", c=P))
-        nc.scalar.dma_start(out=affine_rows[2:3, :], in_=gamma_l.rearrange("(r c) -> r c", c=P))
-        nc.scalar.dma_start(out=affine_rows[3:5, :], in_=beta_u.rearrange("(r c) -> r c", c=P))
-        nc.scalar.dma_start(out=affine_rows[5:6, :], in_=beta_l.rearrange("(r c) -> r c", c=P))
         table_warmer = keep.tile([P, 1], F32)
         nc.scalar.activation(out=table_warmer[:], in_=eps[:], func=ACT.Abs_reciprocal_sqrt)
-        for scales, first, width in ((Wu_scales, 0, 2 * P), (Wl_scales, 2 * P, P)):
-            for quadrant in range(QUADRANTS):
-                nc.gpsimd.dma_start(
-                    out=w_scales[32 * quadrant : 32 * quadrant + 4, :, first : first + width].bitcast(F32),
-                    in_=scales[:, 4 * quadrant : 4 * quadrant + 4, :].rearrange("g r n -> r g n").bitcast(F32),
-                )
 
         xp_rows = keep.tile([P, IMAGES, PASSES, PACK, PIXELS], BF16)
         w_words = keep.tile([P, PASSES, OUT_CHANNELS], U32, align_bytes=64)
@@ -118,6 +108,16 @@ def tile_gnn_kernel(
         )
         load_pixels(1, 0)
         load_pixels(1, 1)
+        for scales, first, width in ((Wu_scales, 0, 2 * P), (Wl_scales, 2 * P, P)):
+            for quadrant in range(QUADRANTS):
+                nc.sync.dma_start(
+                    out=w_scales[32 * quadrant : 32 * quadrant + 4, :, first : first + width].bitcast(I32),
+                    in_=scales[:, 4 * quadrant : 4 * quadrant + 4, :].rearrange("g r n -> r g n").bitcast(I32),
+                )
+        nc.sync.dma_start(out=affine_rows[0:2, :], in_=gamma_u.rearrange("(r c) -> r c", c=P))
+        nc.sync.dma_start(out=affine_rows[2:3, :], in_=gamma_l.rearrange("(r c) -> r c", c=P))
+        nc.sync.dma_start(out=affine_rows[3:5, :], in_=beta_u.rearrange("(r c) -> r c", c=P))
+        nc.sync.dma_start(out=affine_rows[5:6, :], in_=beta_l.rearrange("(r c) -> r c", c=P))
         h0 = keep.tile([P, PIXELS], BF16)
         p0 = keep.tile([P, PIXELS], BF16)
         nc.sync.dma_start(out=h0[:], in_=h_nodes[0].rearrange("b c h w -> (b c) (h w)"))
@@ -155,8 +155,6 @@ def tile_gnn_kernel(
         spread_attention(*units[0])
         spread_attention(*units[1])
 
-        affine_ps = psum.tile([P, P], BF16, tag="y", bufs=Y_BANKS)
-        nc.tensor.transpose(out=affine_ps[:], in_=affine_rows[:], identity=identity[:])
         half_affine = keep.tile([P, 2 * N_PAIRS], F32)
         kept_gamma = keep.tile([P, N_PAIRS], F32)
 
@@ -307,8 +305,6 @@ def tile_gnn_kernel(
 
         regroup(nc.vector.tensor_copy, 0, 0)
         regroup(nc.scalar.copy, 0, 1)
-        nc.scalar.activation(out=half_affine[:], in_=affine_ps[:, 0 : 2 * N_PAIRS], func=ACT.Copy, scale=0.5)
-        nc.scalar.activation(out=kept_gamma[:], in_=affine_ps[:, 0:N_PAIRS], func=ACT.Copy, scale=0.5 * N_TILE)
         for k in range(1, len(pixel_tiles)):
             regroup(nc.scalar.copy, k, 0)
             regroup(nc.scalar.copy, k, 1)
@@ -325,6 +321,10 @@ def tile_gnn_kernel(
             quantise_and_convolve(*units[n - 1])
             if n == 4:
                 scalar_statistics(UPPER, 0)
+                affine_ps = psum.tile([P, P], BF16, tag="y", bufs=Y_BANKS)
+                nc.tensor.transpose(out=affine_ps[:], in_=affine_rows[:], identity=identity[:])
+                nc.scalar.activation(out=half_affine[:], in_=affine_ps[:, 0 : 2 * N_PAIRS], func=ACT.Copy, scale=0.5)
+                nc.scalar.activation(out=kept_gamma[:], in_=affine_ps[:, 0:N_PAIRS], func=ACT.Copy, scale=0.5 * N_TILE)
             if n == 5:
                 scalar_statistics(UPPER, 1)
             if n == 6:

@@ -32,8 +32,8 @@ TUPLE = 3
 EPS = 1e-5
 CHUNKS = PIXELS // P
 SCALAR_TILES = {UPPER: 4, LOWER: 3}
-Y_BANKS = 6
-ATT_BANKS = 2
+Y_BANKS = 5
+ATT_BANKS = 3
 
 FLOPS = 2 * OUT_CHANNELS * CHANNELS * IMAGES * PIXELS
 BYTES = (
@@ -152,8 +152,8 @@ def tile_gnn_kernel(
             att_banks[(product, k)] = att_ps
 
         units = [(UPPER, 0), (LOWER, 0), (UPPER, 1), (LOWER, 1), (UPPER, 2), (UPPER, 3), (LOWER, 2), (LOWER, 3)]
-        spread_attention(*units[0])
-        spread_attention(*units[1])
+        for unit in units[0:ATT_BANKS]:
+            spread_attention(*unit)
 
         half_affine = keep.tile([P, 2 * N_PAIRS], F32)
         kept_gamma = keep.tile([P, N_PAIRS], F32)
@@ -312,30 +312,31 @@ def tile_gnn_kernel(
         weigh(UPPER, 0, 0)
         weigh(LOWER, 0, 0)
         weigh(UPPER, 0, 1)
-        spread_attention(*units[2])
+        spread_attention(*units[ATT_BANKS])
         weigh(LOWER, 0, 1)
-        spread_attention(*units[3])
+        spread_attention(*units[ATT_BANKS + 1])
         quantise_and_convolve(*units[0])
         for n in range(2, len(units)):
             weigh(units[n][0], units[n][1], 0)
             quantise_and_convolve(*units[n - 1])
-            if n == 4:
+            if n == 3:
                 scalar_statistics(UPPER, 0)
+            if n == 4:
+                scalar_statistics(UPPER, 1)
                 affine_ps = psum.tile([P, P], BF16, tag="y", bufs=Y_BANKS)
                 nc.tensor.transpose(out=affine_ps[:], in_=affine_rows[:], identity=identity[:])
                 nc.scalar.activation(out=half_affine[:], in_=affine_ps[:, 0 : 2 * N_PAIRS], func=ACT.Copy, scale=0.5)
                 nc.scalar.activation(out=kept_gamma[:], in_=affine_ps[:, 0:N_PAIRS], func=ACT.Copy, scale=0.5 * N_TILE)
             if n == 5:
-                scalar_statistics(UPPER, 1)
+                scalar_statistics(LOWER, 0)
             if n == 6:
                 scalar_statistics(UPPER, 2)
-                scalar_statistics(LOWER, 0)
             if n == 7:
                 scalar_statistics(UPPER, 3)
                 scalar_statistics(LOWER, 1)
             weigh(units[n][0], units[n][1], 1)
-            if n + 2 < len(units):
-                spread_attention(*units[n + 2])
+            if n + ATT_BANKS < len(units):
+                spread_attention(*units[n + ATT_BANKS])
         mean_and_variance(UPPER)
         gain_and_shift(UPPER)
         quantise_and_convolve(*units[-1])

@@ -168,6 +168,16 @@ def tile_gnn_kernel(
                 in_=xp_rows[:, b, g, :, cols].rearrange("p t (c i) -> p c t i", i=4),
             )
 
+        def regroup_on_gpsimd(k, g, pieces):
+            b, wt = pixel_tiles[k]
+            width = N_TILE // pieces
+            for first in range(wt * N_TILE, (wt + 1) * N_TILE, width):
+                nc.gpsimd.tensor_scalar(
+                    out=xp_grouped[:, b, g, first : first + width, :],
+                    in0=xp_rows[:, b, g, :, first : first + width].rearrange("p t w -> p w t"),
+                    scalar1=1.0, scalar2=0.0, op0=ALU.mult, op1=ALU.add,
+                )
+
         weighted_tiles = {}
 
         def weigh(product, k, g):
@@ -305,7 +315,9 @@ def tile_gnn_kernel(
 
         regroup(nc.vector.tensor_copy, 0, 0)
         regroup(nc.scalar.copy, 0, 1)
-        for k in range(1, len(pixel_tiles)):
+        regroup_on_gpsimd(1, 0, pieces=2)
+        regroup(nc.scalar.copy, 1, 1)
+        for k in range(2, len(pixel_tiles)):
             regroup(nc.scalar.copy, k, 0)
             regroup(nc.scalar.copy, k, 1)
 

@@ -65,13 +65,17 @@ def tile_gnn_kernel(
 
         att_rows = keep.tile([P, P], BF16)
         affine_rows = keep.tile([P, P], BF16)
-        w_scales = keep.tile([P, PASSES, OUT_CHANNELS], U8, align_bytes=64)
+        loaded_scales = {}
+        for product in (UPPER, LOWER):
+            product_scales = keep.tile([P, PASSES, len(PAIRS_OF[product]) * P], U8, name="loaded_scales_%d" % product)
+            loaded_scales[product] = product_scales
         eps = keep.tile([P, 1], F32)
         nc.vector.memset(att_rows[32:64, :].bitcast(I32), 0)
         nc.vector.memset(att_rows[64:128, :].bitcast(I32), 0)
         nc.vector.memset(eps[:], EPS)
         nc.vector.memset(affine_rows[:].bitcast(I32), 0)
-        nc.vector.memset(w_scales[:].rearrange("p g n -> p (g n)").bitcast(I32), 0)
+        for product in (UPPER, LOWER):
+            nc.vector.memset(loaded_scales[product][:].rearrange("p g n -> p (g n)").bitcast(I32), 0)
         identity = keep.tile([P, P], BF16)
         make_identity(nc, identity[:])
         identity_words = keep.tile([P, P], F32)
@@ -84,13 +88,20 @@ def tile_gnn_kernel(
         table_warmer = keep.tile([P, 1], F32)
         nc.scalar.activation(out=table_warmer[:], in_=eps[:], func=ACT.Abs_reciprocal_sqrt)
 
-        xp_rows = keep.tile([P, IMAGES, PASSES, PACK, PIXELS], BF16)
-        w_words = keep.tile([P, PASSES, OUT_CHANNELS], U32, align_bytes=64)
+        xp_rows = {}
+        for k in range(len(pixel_tiles)):
+            for g in range(PASSES):
+                xp_piece = keep.tile([P, PACK, N_TILE], BF16, name="xp_rows_%d_%d" % (k, g))
+                xp_rows[(k, g)] = xp_piece
+        loaded_words = {}
+        for product in (UPPER, LOWER):
+            product_words = keep.tile([P, PASSES, len(PAIRS_OF[product]) * P], U32, name="loaded_words_%d" % product)
+            loaded_words[product] = product_words
 
         def load_pixels(b, wt):
             for g in range(PASSES):
                 nc.sync.dma_start(
-                    out=xp_rows[:, b, g, :, wt * N_TILE : (wt + 1) * N_TILE],
+                    out=xp_rows[(b * PIXEL_TILES + wt, g)][:],
                     in_=xp[b, g * K_PASS : (g + 1) * K_PASS].rearrange("(p t) h w -> p t (h w)", t=PACK)[
                         :, :, wt * N_TILE : (wt + 1) * N_TILE
                     ],
@@ -99,19 +110,19 @@ def tile_gnn_kernel(
         load_pixels(0, 0)
         load_pixels(0, 1)
         nc.sync.dma_start(
-            out=w_words[:, :, 0 : 2 * P].bitcast(I32),
+            out=loaded_words[UPPER][:].bitcast(I32),
             in_=Wu_words.rearrange("g p n t -> p g (n t)").bitcast(I32),
         )
         nc.sync.dma_start(
-            out=w_words[:, :, 2 * P : 3 * P].bitcast(I32),
+            out=loaded_words[LOWER][:].bitcast(I32),
             in_=Wl_words.rearrange("g p n t -> p g (n t)").bitcast(I32),
         )
         load_pixels(1, 0)
         load_pixels(1, 1)
-        for scales, first, width in ((Wu_scales, 0, 2 * P), (Wl_scales, 2 * P, P)):
+        for product, scales in ((UPPER, Wu_scales), (LOWER, Wl_scales)):
             for quadrant in range(QUADRANTS):
                 nc.sync.dma_start(
-                    out=w_scales[32 * quadrant : 32 * quadrant + 4, :, first : first + width].bitcast(I32),
+                    out=loaded_scales[product][32 * quadrant : 32 * quadrant + 4].bitcast(I32),
                     in_=scales[:, 4 * quadrant : 4 * quadrant + 4, :].rearrange("g r n -> r g n").bitcast(I32),
                 )
         nc.sync.dma_start(out=affine_rows[0:2, :], in_=gamma_u.rearrange("(r c) -> r c", c=P))
@@ -126,7 +137,7 @@ def tile_gnn_kernel(
         for pair in range(N_PAIRS):
             for half in range(2):
                 nc.sync.dma_start(
-                    out=p_pairs[half * HID : (half + 1) * HID, pair],
+                    out=p_pairs[half:P:2, pair],
                     in_=p_nodes[1 + 2 * pair + half].rearrange("b c h w -> c b (h w)"),
                 )
 
@@ -155,6 +166,22 @@ def tile_gnn_kernel(
         for unit in units[0:ATT_BANKS]:
             spread_attention(*unit)
 
+        woven_words = {}
+        woven_scales = {}
+        for pair in range(N_PAIRS):
+            pair_words = keep.tile([P, PASSES, P], U32, align_bytes=64, name="woven_words_%d" % pair)
+            pair_scales = keep.tile([P, PASSES, P], U8, align_bytes=64, name="woven_scales_%d" % pair)
+            woven_words[pair] = pair_words
+            woven_scales[pair] = pair_scales
+
+        def weave(woven, loaded, product):
+            for n in range(len(PAIRS_OF[product])):
+                nc.gpsimd.tensor_copy(
+                    out=woven[PAIRS_OF[product][n]][:].rearrange("p g (c h) -> p g c h", h=2),
+                    in_=loaded[product][:, :, n * P : (n + 1) * P].rearrange("p g (h c) -> p g c h", h=2),
+                )
+
+        affine_woven = keep.tile([P, P], BF16)
         half_affine = keep.tile([P, 2 * N_PAIRS], F32)
         kept_gamma = keep.tile([P, N_PAIRS], F32)
 
@@ -165,16 +192,16 @@ def tile_gnn_kernel(
             cols = slice(wt * N_TILE, (wt + 1) * N_TILE)
             copy(
                 out=xp_grouped[:, b, g, cols, :].rearrange("p (c i) t -> p c t i", i=4),
-                in_=xp_rows[:, b, g, :, cols].rearrange("p t (c i) -> p c t i", i=4),
+                in_=xp_rows[(k, g)][:].rearrange("p t (c i) -> p c t i", i=4),
             )
 
         def regroup_on_gpsimd(k, g, pieces):
             b, wt = pixel_tiles[k]
             width = N_TILE // pieces
-            for first in range(wt * N_TILE, (wt + 1) * N_TILE, width):
+            for first in range(0, N_TILE, width):
                 nc.gpsimd.tensor_scalar(
-                    out=xp_grouped[:, b, g, first : first + width, :],
-                    in0=xp_rows[:, b, g, :, first : first + width].rearrange("p t w -> p w t"),
+                    out=xp_grouped[:, b, g, wt * N_TILE + first : wt * N_TILE + first + width, :],
+                    in0=xp_rows[(k, g)][:, :, first : first + width].rearrange("p t w -> p w t"),
                     scalar1=1.0, scalar2=0.0, op0=ALU.mult, op1=ALU.add,
                 )
 
@@ -209,8 +236,8 @@ def tile_gnn_kernel(
                 for g in range(PASSES):
                     nc.tensor.matmul_mx(
                         out=y[:],
-                        lhsT=w_words[:, g, pair * P : (pair + 1) * P].bitcast(FP8X4),
-                        lhsT_scale=w_scales[:, g, pair * P : (pair + 1) * P],
+                        lhsT=woven_words[pair][:, g, :].bitcast(FP8X4),
+                        lhsT_scale=woven_scales[pair][:, g, :],
                         rhs=codes[:, g * N_TILE : (g + 1) * N_TILE].bitcast(FP8X4),
                         rhs_scale=scales[:, g * N_TILE : (g + 1) * N_TILE],
                         start=(g == 0),
@@ -310,13 +337,21 @@ def tile_gnn_kernel(
             for half in range(2):
                 nc.sync.dma_start(
                     out=out[1 + 2 * pair + half, b].rearrange("c h w -> c (h w)")[:, cols],
-                    in_=result[half * HID : (half + 1) * HID, 0 : tiles * N_TILE],
+                    in_=result[half:P:2, 0 : tiles * N_TILE],
                 )
 
         regroup(nc.vector.tensor_copy, 0, 0)
         regroup(nc.scalar.copy, 0, 1)
         regroup_on_gpsimd(1, 0, pieces=2)
         regroup(nc.scalar.copy, 1, 1)
+        for product in (UPPER, LOWER):
+            weave(woven_words, loaded_words, product)
+        for product in (UPPER, LOWER):
+            weave(woven_scales, loaded_scales, product)
+        nc.gpsimd.tensor_copy(
+            out=affine_woven[:].rearrange("p (c h) -> p c h", h=2),
+            in_=affine_rows[:].rearrange("p (h c) -> p c h", h=2),
+        )
         for k in range(2, len(pixel_tiles)):
             regroup(nc.scalar.copy, k, 0)
             regroup(nc.scalar.copy, k, 1)
@@ -336,7 +371,7 @@ def tile_gnn_kernel(
             if n == 4:
                 scalar_statistics(UPPER, 1)
                 affine_ps = psum.tile([P, P], BF16, tag="y", bufs=Y_BANKS)
-                nc.tensor.transpose(out=affine_ps[:], in_=affine_rows[:], identity=identity[:])
+                nc.tensor.transpose(out=affine_ps[:], in_=affine_woven[:], identity=identity[:])
                 nc.scalar.activation(out=half_affine[:], in_=affine_ps[:, 0 : 2 * N_PAIRS], func=ACT.Copy, scale=0.5)
                 nc.scalar.activation(out=kept_gamma[:], in_=affine_ps[:, 0:N_PAIRS], func=ACT.Copy, scale=0.5 * N_TILE)
             if n == 5:

@@ -27,12 +27,15 @@ PAIRS_OF = {UPPER: (0, 1), LOWER: (2,)}
 N_PAIRS = 3
 OUT_CHANNELS = N_PAIRS * P
 QUADRANTS = 4
-STATS = 6
+COUNT = IMAGES * PIXELS
+SUM_COLS = P
+SUM_PARTS = ((0, 1), (2,))
 TUPLE = 3
+STATS = 2 * TUPLE
 EPS = 1e-5
 CHUNKS = PIXELS // P
-SCALAR_TILES = {UPPER: 4, LOWER: 3}
-Y_BANKS = 5
+Y_BANKS = 4
+SUM_BANKS = 1
 ATT_BANKS = 3
 
 FLOPS = 2 * OUT_CHANNELS * CHANNELS * IMAGES * PIXELS
@@ -56,8 +59,7 @@ def tile_gnn_kernel(
         stack.enter_context(tc.manual_schedule())
         keep = stack.enter_context(tc.tile_pool(name="keep", bufs=1))
         products = stack.enter_context(tc.tile_pool(name="products", bufs=3))
-        quantised = stack.enter_context(tc.tile_pool(name="quantised", bufs=4))
-        results = stack.enter_context(tc.tile_pool(name="results", bufs=4))
+        results = stack.enter_context(tc.tile_pool(name="results", bufs=6))
         psum = stack.enter_context(tc.psum_pool(name="psum", bufs=1))
 
         pixel_tiles = [(b, wt) for b in range(IMAGES) for wt in range(PIXEL_TILES)]
@@ -81,7 +83,7 @@ def tile_gnn_kernel(
         identity_words = keep.tile([P, P], F32)
         make_identity(nc, identity_words[:])
 
-        nc.scalar.dma_start(
+        nc.sync.dma_start(
             out=att_rows[0 : 2 * IMAGES * CHUNKS, :],
             in_=h_att[1:3].rearrange("a b o (c h) w -> (a b o c) (h w)", c=CHUNKS),
         )
@@ -144,7 +146,7 @@ def tile_gnn_kernel(
         att_cols_ps = psum.tile([P, P], BF16, tag="y", bufs=Y_BANKS)
         nc.tensor.transpose(out=att_cols_ps[:], in_=att_rows[:], identity=identity[:])
         att_words = keep.tile([P, 2 * IMAGES * CHUNKS, 2], BF16)
-        nc.vector.tensor_copy(
+        nc.scalar.copy(
             out=att_words[:],
             in_=att_cols_ps[:, 0 : 2 * IMAGES * CHUNKS].unsqueeze(2).to_broadcast([P, 2 * IMAGES * CHUNKS, 2]),
         )
@@ -162,7 +164,7 @@ def tile_gnn_kernel(
                 )
             att_banks[(product, k)] = att_ps
 
-        units = [(UPPER, 0), (LOWER, 0), (UPPER, 1), (LOWER, 1), (UPPER, 2), (UPPER, 3), (LOWER, 2), (LOWER, 3)]
+        units = [(UPPER, 0), (LOWER, 0), (UPPER, 1), (UPPER, 2), (UPPER, 3), (LOWER, 1), (LOWER, 2), (LOWER, 3)]
         for unit in units[0:ATT_BANKS]:
             spread_attention(*unit)
 
@@ -183,7 +185,6 @@ def tile_gnn_kernel(
 
         affine_woven = keep.tile([P, P], BF16)
         half_affine = keep.tile([P, 2 * N_PAIRS], F32)
-        kept_gamma = keep.tile([P, N_PAIRS], F32)
 
         xp_grouped = keep.tile([P, IMAGES, PASSES, PIXELS, PACK], BF16)
 
@@ -221,72 +222,172 @@ def tile_gnn_kernel(
                 op=ALU.mult,
             )
 
-        y_banks = {}
+        codes = {}
+        scales = {}
 
-        def quantise_and_convolve(product, k):
-            codes = quantised.tile([P, PASSES * N_TILE], U32, align_bytes=64)
-            scales = quantised.tile([P, PASSES * N_TILE], U8, align_bytes=64)
+        def quantise(product, k):
+            unit_codes = keep.tile([P, PASSES * N_TILE], U32, align_bytes=64, name="codes_%d_%d" % (product, k))
+            unit_scales = keep.tile([P, PASSES * N_TILE], U8, align_bytes=64, name="scales_%d_%d" % (product, k))
             nc.vector.quantize_mx(
-                out=codes[:].bitcast(FP8X4),
-                scales=scales[:],
+                out=unit_codes[:].bitcast(FP8X4),
+                scales=unit_scales[:],
                 in_=weighted_tiles[(product, k)][:].rearrange("p g w t -> p (g w t)"),
             )
-            for pair in PAIRS_OF[product]:
-                y = psum.tile([P, N_TILE], F32, tag="y", bufs=Y_BANKS)
-                for g in range(PASSES):
-                    nc.tensor.matmul_mx(
-                        out=y[:],
-                        lhsT=woven_words[pair][:, g, :].bitcast(FP8X4),
-                        lhsT_scale=woven_scales[pair][:, g, :],
-                        rhs=codes[:, g * N_TILE : (g + 1) * N_TILE].bitcast(FP8X4),
-                        rhs_scale=scales[:, g * N_TILE : (g + 1) * N_TILE],
-                        start=(g == 0),
-                        stop=(g == PASSES - 1),
-                    )
-                y_banks[(pair, k)] = y
+            codes[(product, k)] = unit_codes
+            scales[(product, k)] = unit_scales
 
-        stats_used = {
-            product: SCALAR_TILES[product] * TUPLE + (len(pixel_tiles) - SCALAR_TILES[product]) * STATS
-            for product in (UPPER, LOWER)
-        }
-        stats = keep.tile([P, N_PAIRS, max(stats_used.values())], F32)
-        y_kept = keep.tile([P, N_PAIRS, len(pixel_tiles), N_TILE], F32)
+        def product_of(pair):
+            return UPPER if pair in PAIRS_OF[UPPER] else LOWER
 
-        nc.vector.memset(stats[:], float(N_TILE))
-
-        def scalar_statistics(product, k):
-            for pair in PAIRS_OF[product]:
-                nc.scalar.activation(
-                    out=y_kept[:, pair, k, :], in_=y_banks[(pair, k)][:], func=ACT.Copy, scale=1.0 / N_TILE,
-                    accum_out=stats[:, pair, k * TUPLE + 1 : k * TUPLE + 2],
+        def multiply(bank, pair, pieces):
+            product = product_of(pair)
+            steps = [(piece, g) for piece in pieces for g in range(PASSES)]
+            for n in range(len(steps)):
+                (k, first, width), g = steps[n]
+                cols = slice(g * N_TILE + first, g * N_TILE + first + width)
+                nc.tensor.matmul_mx(
+                    out=bank,
+                    lhsT=woven_words[pair][:, g, :].bitcast(FP8X4),
+                    lhsT_scale=woven_scales[pair][:, g, :],
+                    rhs=codes[(product, k)][:, cols].bitcast(FP8X4),
+                    rhs_scale=scales[(product, k)][:, cols],
+                    start=(n == 0),
+                    stop=(n == len(steps) - 1),
                 )
-            for pair in PAIRS_OF[product]:
+
+        y_banks = {}
+
+        def convolve(pair, k, tag="y", bufs=Y_BANKS):
+            y = psum.tile([P, N_TILE], F32, tag=tag, bufs=bufs)
+            multiply(y[:], pair, [(k, 0, N_TILE)])
+            y_banks[(pair, k)] = y
+
+        half_identity = keep.tile([P, P], BF16)
+        nc.gpsimd.tensor_scalar(
+            out=half_identity[:], in0=identity[:], scalar1=0.5, scalar2=0.0, op0=ALU.mult, op1=ALU.add
+        )
+
+        def average_node0():
+            node0 = keep.tile([P, PIXELS], F32)
+            for first in range(0, PIXELS, N_TILE):
+                cols = slice(first, first + N_TILE)
+                half_sum = psum.tile([P, N_TILE], F32, tag="y", bufs=Y_BANKS)
+                nc.tensor.matmul(out=half_sum[:], lhsT=half_identity[:], rhs=h0[:, cols], start=True, stop=False)
+                nc.tensor.matmul(out=half_sum[:], lhsT=half_identity[:], rhs=p0[:, cols], start=False, stop=True)
+                nc.scalar.copy(out=node0[:, cols], in_=half_sum[:])
+            nc.sync.dma_start(out=out[0].rearrange("b c h w -> (b c) (h w)"), in_=node0[:])
+
+        upper = slice(PAIRS_OF[UPPER][0], PAIRS_OF[UPPER][-1] + 1)
+        n_upper = len(PAIRS_OF[UPPER])
+        sums = psum.tile([P, n_upper, len(SUM_PARTS), SUM_COLS], F32, tag="sums", bufs=SUM_BANKS)
+
+        def sum_pixels(part):
+            for pair in PAIRS_OF[UPPER]:
+                multiply(
+                    sums[:, pair, part, :], pair,
+                    [(k, first, SUM_COLS) for k in SUM_PARTS[part] for first in range(0, N_TILE, SUM_COLS)],
+                )
+
+        pilot = keep.tile([P, n_upper], F32)
+        minus_pilot = keep.tile([P, n_upper], F32)
+        minus_pilot_gamma = keep.tile([P, n_upper], F32)
+        squares = keep.tile([P, n_upper, len(pixel_tiles)], F32)
+
+        def take_pilot():
+            for pair in PAIRS_OF[UPPER]:
                 unused = results.tile([P, N_TILE], BF16)
                 nc.scalar.activation(
-                    out=unused[:], in_=y_kept[:, pair, k, :], func=ACT.Square, scale=-float(N_TILE),
-                    bias=stats[:, pair, k * TUPLE + 1 : k * TUPLE + 2],
-                    accum_out=stats[:, pair, k * TUPLE + 2 : k * TUPLE + 3],
+                    out=unused[:, 0:SUM_COLS], in_=y_banks[(pair, 0)][:, 0:SUM_COLS], func=ACT.Copy,
+                    scale=1.0 / SUM_COLS, accum_out=pilot[:, pair : pair + 1],
+                )
+            nc.scalar.activation(
+                out=minus_pilot[:], in_=pilot[:], func=ACT.Copy, scale=-1.0 / (len(SUM_PARTS) * SUM_COLS)
+            )
+
+        def take_squares(k):
+            for pair in PAIRS_OF[UPPER]:
+                unused = results.tile([P, N_TILE], BF16)
+                nc.scalar.activation(
+                    out=unused[:], in_=y_banks[(pair, k)][:], func=ACT.Square, scale=-1.0,
+                    bias=pilot[:, pair : pair + 1], accum_out=squares[:, pair, k : k + 1],
                 )
 
-        def vector_statistics(product, k):
-            first = SCALAR_TILES[product] * TUPLE + (k - SCALAR_TILES[product]) * STATS
-            for pair in PAIRS_OF[product]:
-                nc.vector.bn_stats(out=stats[:, pair, first : first + STATS], in_=y_banks[(pair, k)][:])
+        tuples = keep.tile([P, last * TUPLE + STATS], F32)
+        nc.vector.memset(tuples[:], float(N_TILE))
 
-        mean_var = keep.tile([P, N_PAIRS, 2], F32)
+        def take_tuple(k):
+            (pair,) = PAIRS_OF[LOWER]
+            mean = tuples[:, k * TUPLE + 1 : k * TUPLE + 2]
+            unused = results.tile([P, N_TILE], BF16)
+            nc.scalar.activation(
+                out=unused[:], in_=y_banks[(pair, k)][:], func=ACT.Copy, scale=1.0 / N_TILE, accum_out=mean
+            )
+            unused = results.tile([P, N_TILE], BF16)
+            nc.scalar.activation(
+                out=unused[:], in_=y_banks[(pair, k)][:], func=ACT.Square, scale=-1.0, bias=mean,
+                accum_out=tuples[:, k * TUPLE + 2 : k * TUPLE + 3],
+            )
+
+        mean_less_pilot = keep.tile([P, n_upper], F32)
+        square_sum = keep.tile([P, n_upper], F32)
+        variance = keep.tile([P, n_upper], F32)
+        mean_var = keep.tile([P, 2], F32)
         minus_mean_gamma = keep.tile([P, N_PAIRS], F32)
         inv_std = keep.tile([P, N_PAIRS], F32)
         gain = keep.tile([P, N_PAIRS], F32)
-        kept_gain = keep.tile([P, N_PAIRS], F32)
         shift = keep.tile([P, N_PAIRS], F32)
 
-        def mean_and_variance(product):
-            pairs = PAIRS_OF[product]
-            these = slice(pairs[0], pairs[-1] + 1)
-            for pair in pairs:
-                nc.vector.bn_aggr(out=mean_var[:, pair, :], in_=stats[:, pair, 0 : stats_used[product]])
+        mean_parts = keep.tile([P, n_upper, 2], F32)
+
+        def take_mean_of_sums():
+            width = len(SUM_PARTS) * SUM_COLS
+            for pair in PAIRS_OF[UPPER]:
+                unused = results.tile([P, N_TILE], BF16)
+                nc.scalar.activation(
+                    out=unused[:, 0:width], in_=sums[:, pair].rearrange("p s w -> p (s w)"),
+                    func=ACT.Identity, scale=1.0 / COUNT, bias=minus_pilot[:, pair : pair + 1],
+                    accum_out=mean_parts[:, pair, 0:1],
+                )
+
+        def take_mean_of_last():
+            for pair in PAIRS_OF[UPPER]:
+                unused = results.tile([P, N_TILE], BF16)
+                nc.scalar.activation(
+                    out=unused[:], in_=y_banks[(pair, last)][:], func=ACT.Copy, scale=1.0 / COUNT,
+                    accum_out=mean_parts[:, pair, 1:2],
+                )
+
+        def pilot_and_gamma():
             nc.vector.scalar_tensor_tensor(
-                out=minus_mean_gamma[:, these], in0=mean_var[:, these, 0], scalar=-1.0, in1=half_affine[:, these],
+                out=minus_pilot_gamma[:], in0=pilot[:], scalar=-1.0, in1=half_affine[:, upper],
+                op0=ALU.mult, op1=ALU.mult,
+            )
+
+        def upper_mean_and_variance():
+            nc.vector.tensor_reduce(out=mean_less_pilot[:], in_=mean_parts[:], axis=mybir.AxisListType.X, op=ALU.add)
+            nc.vector.tensor_reduce(out=square_sum[:], in_=squares[:], axis=mybir.AxisListType.X, op=ALU.add)
+            nc.vector.scalar_tensor_tensor(
+                out=variance[:], in0=mean_less_pilot[:], scalar=-1.0, in1=mean_less_pilot[:],
+                op0=ALU.mult, op1=ALU.mult,
+            )
+            nc.vector.scalar_tensor_tensor(
+                out=minus_mean_gamma[:, upper], in0=mean_less_pilot[:], scalar=-1.0, in1=half_affine[:, upper],
+                op0=ALU.mult, op1=ALU.mult,
+            )
+            nc.vector.scalar_tensor_tensor(
+                out=variance[:], in0=square_sum[:], scalar=1.0 / COUNT, in1=variance[:],
+                op0=ALU.mult, op1=ALU.add,
+            )
+            nc.vector.tensor_tensor(
+                out=minus_mean_gamma[:, upper], in0=minus_mean_gamma[:, upper], in1=minus_pilot_gamma[:], op=ALU.add
+            )
+
+        def lower_mean_and_variance():
+            (pair,) = PAIRS_OF[LOWER]
+            one = slice(pair, pair + 1)
+            nc.vector.bn_aggr(out=mean_var[:], in_=tuples[:])
+            nc.vector.scalar_tensor_tensor(
+                out=minus_mean_gamma[:, one], in0=mean_var[:, 0:1], scalar=-1.0, in1=half_affine[:, one],
                 op0=ALU.mult, op1=ALU.mult,
             )
 
@@ -294,34 +395,24 @@ def tile_gnn_kernel(
             pairs = PAIRS_OF[product]
             these = slice(pairs[0], pairs[-1] + 1)
             nc.scalar.activation(
-                out=inv_std[:, these], in_=mean_var[:, these, 1], func=ACT.Abs_reciprocal_sqrt, bias=eps[:]
+                out=inv_std[:, these], in_=variance[:] if product == UPPER else mean_var[:, 1:2],
+                func=ACT.Abs_reciprocal_sqrt, bias=eps[:],
             )
             for pair in pairs:
                 one = slice(pair, pair + 1)
-                nc.scalar.activation(out=kept_gain[:, one], in_=kept_gamma[:, one], func=ACT.Copy, scale=inv_std[:, one])
+                nc.scalar.activation(out=gain[:, one], in_=half_affine[:, one], func=ACT.Copy, scale=inv_std[:, one])
                 nc.scalar.activation(
                     out=shift[:, one], in_=minus_mean_gamma[:, one], func=ACT.Identity, scale=inv_std[:, one],
                     bias=half_affine[:, N_PAIRS + pair : N_PAIRS + pair + 1],
                 )
 
-        def plain_gain(product):
-            for pair in PAIRS_OF[product]:
-                one = slice(pair, pair + 1)
-                nc.scalar.activation(out=gain[:, one], in_=half_affine[:, one], func=ACT.Copy, scale=inv_std[:, one])
-
         half_relus = {}
 
         def normalise(pair, k, tiles):
             half_relu = results.tile([P, 2 * N_TILE], F32)
-            if k < SCALAR_TILES[UPPER if pair in PAIRS_OF[UPPER] else LOWER]:
+            for i in range(tiles):
                 nc.scalar.activation(
-                    out=half_relu[:, 0 : tiles * N_TILE],
-                    in_=y_kept[:, pair, k : k + tiles, :].rearrange("p k w -> p (k w)"), func=ACT.Relu,
-                    bias=shift[:, pair : pair + 1], scale=kept_gain[:, pair : pair + 1],
-                )
-            else:
-                nc.scalar.activation(
-                    out=half_relu[:, 0:N_TILE], in_=y_banks[(pair, k)][:], func=ACT.Relu,
+                    out=half_relu[:, i * N_TILE : (i + 1) * N_TILE], in_=y_banks[(pair, k + i)][:], func=ACT.Relu,
                     bias=shift[:, pair : pair + 1], scale=gain[:, pair : pair + 1],
                 )
             half_relus[(pair, k)] = half_relu
@@ -352,9 +443,9 @@ def tile_gnn_kernel(
             out=affine_woven[:].rearrange("p (c h) -> p c h", h=2),
             in_=affine_rows[:].rearrange("p (h c) -> p c h", h=2),
         )
-        for k in range(2, len(pixel_tiles)):
-            regroup(nc.scalar.copy, k, 0)
-            regroup(nc.scalar.copy, k, 1)
+        regroup(nc.scalar.copy, 2, 0)
+        regroup(nc.scalar.copy, 2, 1)
+        regroup(nc.scalar.copy, 3, 0)
 
         weigh(UPPER, 0, 0)
         weigh(LOWER, 0, 0)
@@ -362,52 +453,70 @@ def tile_gnn_kernel(
         spread_attention(*units[ATT_BANKS])
         weigh(LOWER, 0, 1)
         spread_attention(*units[ATT_BANKS + 1])
-        quantise_and_convolve(*units[0])
+        quantise(*units[0])
+        for pair in PAIRS_OF[UPPER]:
+            convolve(pair, 0)
+        take_pilot()
+        take_squares(0)
+        regroup(nc.scalar.copy, 3, 1)
+
+        kept_tiles = (2, 3)
+        (lower_pair,) = PAIRS_OF[LOWER]
+        upper_runs = [(pair, k, PIXEL_TILES) for k in range(0, len(pixel_tiles), PIXEL_TILES) for pair in PAIRS_OF[UPPER]]
+
+        def convolve_and_normalise(pair, k, tiles):
+            for i in range(tiles):
+                convolve(pair, k + i)
+            normalise(pair, k, tiles)
+
         for n in range(2, len(units)):
             weigh(units[n][0], units[n][1], 0)
-            quantise_and_convolve(*units[n - 1])
-            if n == 3:
-                scalar_statistics(UPPER, 0)
-            if n == 4:
-                scalar_statistics(UPPER, 1)
-                affine_ps = psum.tile([P, P], BF16, tag="y", bufs=Y_BANKS)
-                nc.tensor.transpose(out=affine_ps[:], in_=affine_woven[:], identity=identity[:])
-                nc.scalar.activation(out=half_affine[:], in_=affine_ps[:, 0 : 2 * N_PAIRS], func=ACT.Copy, scale=0.5)
-                nc.scalar.activation(out=kept_gamma[:], in_=affine_ps[:, 0:N_PAIRS], func=ACT.Copy, scale=0.5 * N_TILE)
-            if n == 5:
-                scalar_statistics(LOWER, 0)
-            if n == 6:
-                scalar_statistics(UPPER, 2)
+            product, k = units[n - 1]
+            quantise(product, k)
             if n == 7:
-                scalar_statistics(UPPER, 3)
-                scalar_statistics(LOWER, 1)
+                convolve_and_normalise(*upper_runs[0])
+                convolve_and_normalise(*upper_runs[1])
+                average_node0()
+            for pair in PAIRS_OF[product]:
+                if product == LOWER and k in kept_tiles:
+                    convolve(pair, k, "att", ATT_BANKS)
+                else:
+                    convolve(pair, k)
+            if product == UPPER:
+                take_squares(k)
+            else:
+                take_tuple(k)
             weigh(units[n][0], units[n][1], 1)
             if n + ATT_BANKS < len(units):
                 spread_attention(*units[n + ATT_BANKS])
-        mean_and_variance(UPPER)
-        gain_and_shift(UPPER)
-        quantise_and_convolve(*units[-1])
-
-        half_h0 = keep.tile([P, PIXELS], BF16)
-        nc.gpsimd.tensor_scalar(out=half_h0[:], in0=h0[:], scalar1=0.5, scalar2=0.0, op0=ALU.mult, op1=ALU.add)
-        node0 = keep.tile([P, PIXELS], F32)
-        nc.vector.scalar_tensor_tensor(
-            out=node0[:], in0=p0[:], scalar=0.5, in1=half_h0[:], op0=ALU.mult, op1=ALU.add
-        )
-        nc.sync.dma_start(out=out[0].rearrange("b c h w -> (b c) (h w)"), in_=node0[:])
-
-        upper_runs = [(pair, k, PIXEL_TILES) for k in range(0, len(pixel_tiles), PIXEL_TILES) for pair in PAIRS_OF[UPPER]]
-        lower_runs = [(PAIRS_OF[LOWER][0], 0, PIXEL_TILES), (PAIRS_OF[LOWER][0], 2, 1), (PAIRS_OF[LOWER][0], 3, 1)]
-        vector_statistics(LOWER, last)
-        normalise(*upper_runs[0])
+            if n == 3:
+                sum_pixels(0)
+            if n == 4:
+                sum_pixels(1)
+                affine_ps = psum.tile([P, P], BF16, tag="y", bufs=Y_BANKS)
+                nc.tensor.transpose(out=affine_ps[:], in_=affine_woven[:], identity=identity[:])
+                nc.scalar.activation(out=half_affine[:], in_=affine_ps[:, 0 : 2 * N_PAIRS], func=ACT.Copy, scale=0.5)
+                take_mean_of_sums()
+            if n == 5:
+                take_mean_of_last()
+            if n == 6:
+                pilot_and_gamma()
+                upper_mean_and_variance()
+                gain_and_shift(UPPER)
+        convolve_and_normalise(*upper_runs[2])
+        quantise(*units[-1])
         add_node(*upper_runs[0])
-        scalar_statistics(LOWER, 2)
-        mean_and_variance(LOWER)
-        for run in upper_runs[1:]:
-            normalise(*run)
-            add_node(*run)
+        convolve(lower_pair, last, "att", ATT_BANKS)
+        add_node(*upper_runs[1])
+        nc.vector.bn_stats(out=tuples[:, last * TUPLE : last * TUPLE + STATS], in_=y_banks[(lower_pair, last)][:])
+        lower_mean_and_variance()
+        convolve_and_normalise(*upper_runs[3])
         gain_and_shift(LOWER)
-        plain_gain(LOWER)
-        for run in lower_runs:
-            normalise(*run)
-            add_node(*run)
+        add_node(*upper_runs[2])
+        add_node(*upper_runs[3])
+
+        convolve_and_normalise(lower_pair, 0, PIXEL_TILES)
+        add_node(lower_pair, 0, PIXEL_TILES)
+        for k in kept_tiles:
+            normalise(lower_pair, k, 1)
+            add_node(lower_pair, k, 1)

@@ -109,6 +109,13 @@ def tile_gnn_kernel(
                     ],
                 )
 
+        def load_scales(product, scales):
+            for quadrant in range(QUADRANTS):
+                nc.sync.dma_start(
+                    out=loaded_scales[product][32 * quadrant : 32 * quadrant + 4].bitcast(I32),
+                    in_=scales[:, 4 * quadrant : 4 * quadrant + 4, :].rearrange("g r n -> r g n").bitcast(I32),
+                )
+
         load_pixels(0, 0)
         load_pixels(0, 1)
         nc.sync.dma_start(
@@ -120,13 +127,9 @@ def tile_gnn_kernel(
             in_=Wl_words.rearrange("g p n t -> p g (n t)").bitcast(I32),
         )
         load_pixels(1, 0)
+        load_scales(UPPER, Wu_scales)
         load_pixels(1, 1)
-        for product, scales in ((UPPER, Wu_scales), (LOWER, Wl_scales)):
-            for quadrant in range(QUADRANTS):
-                nc.sync.dma_start(
-                    out=loaded_scales[product][32 * quadrant : 32 * quadrant + 4].bitcast(I32),
-                    in_=scales[:, 4 * quadrant : 4 * quadrant + 4, :].rearrange("g r n -> r g n").bitcast(I32),
-                )
+        load_scales(LOWER, Wl_scales)
         nc.sync.dma_start(out=affine_rows[0:2, :], in_=gamma_u.rearrange("(r c) -> r c", c=P))
         nc.sync.dma_start(out=affine_rows[2:3, :], in_=gamma_l.rearrange("(r c) -> r c", c=P))
         nc.sync.dma_start(out=affine_rows[3:5, :], in_=beta_u.rearrange("(r c) -> r c", c=P))
@@ -194,6 +197,13 @@ def tile_gnn_kernel(
             copy(
                 out=xp_grouped[:, b, g, cols, :].rearrange("p (c i) t -> p c t i", i=4),
                 in_=xp_rows[(k, g)][:].rearrange("p t (c i) -> p c t i", i=4),
+            )
+
+        def regroup_pixels(copy, k, g, first, last_pixel):
+            b, wt = pixel_tiles[k]
+            copy(
+                out=xp_grouped[:, b, g, wt * N_TILE + first : wt * N_TILE + last_pixel, :].rearrange("p (c i) t -> p c t i", i=4),
+                in_=xp_rows[(k, g)][:, :, first:last_pixel].rearrange("p t (c i) -> p c t i", i=4),
             )
 
         def regroup_on_gpsimd(k, g, pieces):
@@ -431,8 +441,14 @@ def tile_gnn_kernel(
                     in_=result[half:P:2, 0 : tiles * N_TILE],
                 )
 
-        regroup(nc.vector.tensor_copy, 0, 0)
-        regroup(nc.scalar.copy, 0, 1)
+        regroup_pixels(nc.vector.tensor_copy, 0, 0, 0, N_TILE - 128)
+        regroup_pixels(nc.scalar.copy, 0, 0, N_TILE - 128, N_TILE)
+        regroup_pixels(nc.scalar.copy, 0, 1, 0, N_TILE - 128)
+        nc.gpsimd.tensor_scalar(
+            out=xp_grouped[:, 0, 1, N_TILE - 128 : N_TILE, :],
+            in0=xp_rows[(0, 1)][:, :, N_TILE - 128 :].rearrange("p t w -> p w t"),
+            scalar1=1.0, scalar2=0.0, op0=ALU.mult, op1=ALU.add,
+        )
         regroup_on_gpsimd(1, 0, pieces=2)
         regroup(nc.scalar.copy, 1, 1)
         for product in (UPPER, LOWER):
@@ -458,7 +474,7 @@ def tile_gnn_kernel(
             convolve(pair, 0)
         take_pilot()
         take_squares(0)
-        regroup(nc.scalar.copy, 3, 1)
+        regroup_pixels(nc.scalar.copy, 3, 1, 0, N_TILE - 256)
 
         kept_tiles = (2, 3)
         (lower_pair,) = PAIRS_OF[LOWER]
@@ -486,6 +502,8 @@ def tile_gnn_kernel(
                 take_squares(k)
             else:
                 take_tuple(k)
+            if n == 4:
+                regroup_pixels(nc.vector.tensor_copy, 3, 1, N_TILE - 256, N_TILE)
             weigh(units[n][0], units[n][1], 1)
             if n + ATT_BANKS < len(units):
                 spread_attention(*units[n + ATT_BANKS])

from contextlib import ExitStack

import concourse.mybir as mybir
from concourse.masks import make_identity

F32 = mybir.dt.float32
BF16 = mybir.dt.bfloat16
I32 = mybir.dt.int32
U32 = mybir.dt.uint32
U8 = mybir.dt.uint8
FP8X4 = mybir.dt.float8_e4m3fn_x4
ALU = mybir.AluOpType
ACT = mybir.ActivationFunctionType

P = 128
PACK = 4
K_PASS = P * PACK
IMAGES = 2
CHANNELS = 1024
PASSES = CHANNELS // K_PASS
HID = 64
PIXELS = 32 * 32
N_TILE = 512
PIXEL_TILES = PIXELS // N_TILE
UPPER, LOWER = 0, 1
PAIRS_OF = {UPPER: (0, 1), LOWER: (2,)}
N_PAIRS = 3
OUT_CHANNELS = N_PAIRS * P
QUADRANTS = 4
COUNT = IMAGES * PIXELS
SUM_COLS = P
SUM_PARTS = ((0, 1), (2,))
TUPLE = 3
STATS = 2 * TUPLE
EPS = 1e-5
CHUNKS = PIXELS // P
Y_BANKS = 4
SUM_BANKS = 1
ATT_BANKS = 3

FLOPS = 2 * OUT_CHANNELS * CHANNELS * IMAGES * PIXELS
BYTES = (
    2 * (7 + 1) * IMAGES * HID * PIXELS
    + 2 * IMAGES * CHANNELS * PIXELS
    + 2 * 2 * IMAGES * PIXELS
    + OUT_CHANNELS * CHANNELS + OUT_CHANNELS * CHANNELS // 32
    + 2 * 2 * OUT_CHANNELS
    + 4 * 7 * IMAGES * HID * PIXELS
)


def tile_gnn_kernel(
    tc, p_nodes, h_nodes, f_nodes, xp, h_att,
    Wu_words, Wu_scales, Wl_words, Wl_scales,
    gamma_u, beta_u, gamma_l, beta_l, out,
):
    nc = tc.nc
    with ExitStack() as stack:
        stack.enter_context(tc.manual_schedule())
        keep = stack.enter_context(tc.tile_pool(name="keep", bufs=1))
        products = stack.enter_context(tc.tile_pool(name="products", bufs=3))
        results = stack.enter_context(tc.tile_pool(name="results", bufs=6))
        psum = stack.enter_context(tc.psum_pool(name="psum", bufs=1))

        pixel_tiles = [(b, wt) for b in range(IMAGES) for wt in range(PIXEL_TILES)]
        last = len(pixel_tiles) - 1

        att_rows = keep.tile([P, P], BF16)
        affine_rows = keep.tile([P, P], BF16)
        loaded_scales = {}
        for product in (UPPER, LOWER):
            product_scales = keep.tile([P, PASSES, len(PAIRS_OF[product]) * P], U8, name="loaded_scales_%d" % product)
            loaded_scales[product] = product_scales
        eps = keep.tile([P, 1], F32)
        nc.vector.memset(att_rows[32:64, :].bitcast(I32), 0)
        nc.vector.memset(att_rows[64:128, :].bitcast(I32), 0)
        nc.vector.memset(eps[:], EPS)
        nc.vector.memset(affine_rows[:].bitcast(I32), 0)
        for product in (UPPER, LOWER):
            nc.vector.memset(loaded_scales[product][:].rearrange("p g n -> p (g n)").bitcast(I32), 0)
        identity = keep.tile([P, P], BF16)
        make_identity(nc, identity[:])
        identity_words = keep.tile([P, P], F32)
        make_identity(nc, identity_words[:])

        nc.sync.dma_start(
            out=att_rows[0 : 2 * IMAGES * CHUNKS, :],
            in_=h_att[1:3].rearrange("a b o (c h) w -> (a b o c) (h w)", c=CHUNKS),
        )
        table_warmer = keep.tile([P, 1], F32)
        nc.scalar.activation(out=table_warmer[:], in_=eps[:], func=ACT.Abs_reciprocal_sqrt)

        xp_rows = {}
        for k in range(len(pixel_tiles)):
            for g in range(PASSES):
                xp_piece = keep.tile([P, PACK, N_TILE], BF16, name="xp_rows_%d_%d" % (k, g))
                xp_rows[(k, g)] = xp_piece
        loaded_words = {}
        for product in (UPPER, LOWER):
            product_words = keep.tile([P, PASSES, len(PAIRS_OF[product]) * P], U32, name="loaded_words_%d" % product)
            loaded_words[product] = product_words

        def load_pixels(b, wt):
            for g in range(PASSES):
                nc.sync.dma_start(
                    out=xp_rows[(b * PIXEL_TILES + wt, g)][:],
                    in_=xp[b, g * K_PASS : (g + 1) * K_PASS].rearrange("(p t) h w -> p t (h w)", t=PACK)[
                        :, :, wt * N_TILE : (wt + 1) * N_TILE
                    ],
                )

        def load_scales(product, scales):
            for quadrant in range(QUADRANTS):
                nc.sync.dma_start(
                    out=loaded_scales[product][32 * quadrant : 32 * quadrant + 4].bitcast(I32),
                    in_=scales[:, 4 * quadrant : 4 * quadrant + 4, :].rearrange("g r n -> r g n").bitcast(I32),
                )

        load_pixels(0, 0)
        load_pixels(0, 1)
        nc.sync.dma_start(
            out=loaded_words[UPPER][:].bitcast(I32),
            in_=Wu_words.rearrange("g p n t -> p g (n t)").bitcast(I32),
        )
        nc.sync.dma_start(
            out=loaded_words[LOWER][:].bitcast(I32),
            in_=Wl_words.rearrange("g p n t -> p g (n t)").bitcast(I32),
        )
        load_pixels(1, 0)
        load_scales(UPPER, Wu_scales)
        load_pixels(1, 1)
        load_scales(LOWER, Wl_scales)
        nc.sync.dma_start(out=affine_rows[0:2, :], in_=gamma_u.rearrange("(r c) -> r c", c=P))
        nc.sync.dma_start(out=affine_rows[2:3, :], in_=gamma_l.rearrange("(r c) -> r c", c=P))
        nc.sync.dma_start(out=affine_rows[3:5, :], in_=beta_u.rearrange("(r c) -> r c", c=P))
        nc.sync.dma_start(out=affine_rows[5:6, :], in_=beta_l.rearrange("(r c) -> r c", c=P))
        h0 = keep.tile([P, PIXELS], BF16)
        p0 = keep.tile([P, PIXELS], BF16)
        nc.sync.dma_start(out=h0[:], in_=h_nodes[0].rearrange("b c h w -> (b c) (h w)"))
        nc.sync.dma_start(out=p0[:], in_=p_nodes[0].rearrange("b c h w -> (b c) (h w)"))
        p_pairs = keep.tile([P, N_PAIRS, IMAGES, PIXELS], BF16)
        for pair in range(N_PAIRS):
            for half in range(2):
                nc.sync.dma_start(
                    out=p_pairs[half:P:2, pair],
                    in_=p_nodes[1 + 2 * pair + half].rearrange("b c h w -> c b (h w)"),
                )

        att_cols_ps = psum.tile([P, P], BF16, tag="y", bufs=Y_BANKS)
        nc.tensor.transpose(out=att_cols_ps[:], in_=att_rows[:], identity=identity[:])
        att_words = keep.tile([P, 2 * IMAGES * CHUNKS, 2], BF16)
        nc.scalar.copy(
            out=att_words[:],
            in_=att_cols_ps[:, 0 : 2 * IMAGES * CHUNKS].unsqueeze(2).to_broadcast([P, 2 * IMAGES * CHUNKS, 2]),
        )
        att_banks = {}

        def spread_attention(product, k):
            b, wt = pixel_tiles[k]
            att_ps = psum.tile([P, N_TILE], F32, tag="att", bufs=ATT_BANKS)
            for c in range(N_TILE // P):
                j = (product * IMAGES + b) * CHUNKS + wt * (N_TILE // P) + c
                nc.tensor.transpose(
                    out=att_ps[:, c * P : (c + 1) * P],
                    in_=att_words[:].rearrange("p j e -> p (j e)").bitcast(F32)[:, j : j + 1].to_broadcast([P, P]),
                    identity=identity_words[:],
                )
            att_banks[(product, k)] = att_ps

        units = [(UPPER, 0), (LOWER, 0), (UPPER, 1), (UPPER, 2), (UPPER, 3), (LOWER, 1), (LOWER, 2), (LOWER, 3)]
        for unit in units[0:ATT_BANKS]:
            spread_attention(*unit)

        woven_words = {}
        woven_scales = {}
        for pair in range(N_PAIRS):
            pair_words = keep.tile([P, PASSES, P], U32, align_bytes=64, name="woven_words_%d" % pair)
            pair_scales = keep.tile([P, PASSES, P], U8, align_bytes=64, name="woven_scales_%d" % pair)
            woven_words[pair] = pair_words
            woven_scales[pair] = pair_scales

        def weave(woven, loaded, product):
            for n in range(len(PAIRS_OF[product])):
                nc.gpsimd.tensor_copy(
                    out=woven[PAIRS_OF[product][n]][:].rearrange("p g (c h) -> p g c h", h=2),
                    in_=loaded[product][:, :, n * P : (n + 1) * P].rearrange("p g (h c) -> p g c h", h=2),
                )

        affine_woven = keep.tile([P, P], BF16)
        half_affine = keep.tile([P, 2 * N_PAIRS], F32)

        xp_grouped = keep.tile([P, IMAGES, PASSES, PIXELS, PACK], BF16)

        def regroup(copy, k, g):
            b, wt = pixel_tiles[k]
            cols = slice(wt * N_TILE, (wt + 1) * N_TILE)
            copy(
                out=xp_grouped[:, b, g, cols, :].rearrange("p (c i) t -> p c t i", i=4),
                in_=xp_rows[(k, g)][:].rearrange("p t (c i) -> p c t i", i=4),
            )

        def regroup_pixels(copy, k, g, first, last_pixel):
            b, wt = pixel_tiles[k]
            copy(
                out=xp_grouped[:, b, g, wt * N_TILE + first : wt * N_TILE + last_pixel, :].rearrange("p (c i) t -> p c t i", i=4),
                in_=xp_rows[(k, g)][:, :, first:last_pixel].rearrange("p t (c i) -> p c t i", i=4),
            )

        def regroup_on_gpsimd(k, g, pieces):
            b, wt = pixel_tiles[k]
            width = N_TILE // pieces
            for first in range(0, N_TILE, width):
                nc.gpsimd.tensor_scalar(
                    out=xp_grouped[:, b, g, wt * N_TILE + first : wt * N_TILE + first + width, :],
                    in0=xp_rows[(k, g)][:, :, first : first + width].rearrange("p t w -> p w t"),
                    scalar1=1.0, scalar2=0.0, op0=ALU.mult, op1=ALU.add,
                )

        weighted_tiles = {}

        def weigh(product, k, g):
            b, wt = pixel_tiles[k]
            if (product, k) not in weighted_tiles:
                weighted = products.tile([P, PASSES, N_TILE, PACK], BF16, align_bytes=64)
                weighted_tiles[(product, k)] = weighted
            cols = slice(wt * N_TILE, (wt + 1) * N_TILE)
            nc.vector.tensor_tensor(
                out=weighted_tiles[(product, k)][:, g].rearrange("p w (u e) -> p w u e", e=2),
                in0=xp_grouped[:, b, g, cols, :].rearrange("p w (u e) -> p w u e", e=2),
                in1=att_banks[(product, k)][:].bitcast(BF16).rearrange("p (w e) -> p w e", e=2)
                .unsqueeze(2).to_broadcast([P, N_TILE, 2, 2]),
                op=ALU.mult,
            )

        codes = {}
        scales = {}

        def quantise(product, k):
            unit_codes = keep.tile([P, PASSES * N_TILE], U32, align_bytes=64, name="codes_%d_%d" % (product, k))
            unit_scales = keep.tile([P, PASSES * N_TILE], U8, align_bytes=64, name="scales_%d_%d" % (product, k))
            nc.vector.quantize_mx(
                out=unit_codes[:].bitcast(FP8X4),
                scales=unit_scales[:],
                in_=weighted_tiles[(product, k)][:].rearrange("p g w t -> p (g w t)"),
            )
            codes[(product, k)] = unit_codes
            scales[(product, k)] = unit_scales

        def product_of(pair):
            return UPPER if pair in PAIRS_OF[UPPER] else LOWER

        def multiply(bank, pair, pieces):
            product = product_of(pair)
            steps = [(piece, g) for piece in pieces for g in range(PASSES)]
            for n in range(len(steps)):
                (k, first, width), g = steps[n]
                cols = slice(g * N_TILE + first, g * N_TILE + first + width)
                nc.tensor.matmul_mx(
                    out=bank,
                    lhsT=woven_words[pair][:, g, :].bitcast(FP8X4),
                    lhsT_scale=woven_scales[pair][:, g, :],
                    rhs=codes[(product, k)][:, cols].bitcast(FP8X4),
                    rhs_scale=scales[(product, k)][:, cols],
                    start=(n == 0),
                    stop=(n == len(steps) - 1),
                )

        y_banks = {}

        def convolve(pair, k, tag="y", bufs=Y_BANKS):
            y = psum.tile([P, N_TILE], F32, tag=tag, bufs=bufs)
            multiply(y[:], pair, [(k, 0, N_TILE)])
            y_banks[(pair, k)] = y

        half_identity = keep.tile([P, P], BF16)
        nc.gpsimd.tensor_scalar(
            out=half_identity[:], in0=identity[:], scalar1=0.5, scalar2=0.0, op0=ALU.mult, op1=ALU.add
        )

        def average_node0():
            node0 = keep.tile([P, PIXELS], F32)
            for first in range(0, PIXELS, N_TILE):
                cols = slice(first, first + N_TILE)
                half_sum = psum.tile([P, N_TILE], F32, tag="y", bufs=Y_BANKS)
                nc.tensor.matmul(out=half_sum[:], lhsT=half_identity[:], rhs=h0[:, cols], start=True, stop=False)
                nc.tensor.matmul(out=half_sum[:], lhsT=half_identity[:], rhs=p0[:, cols], start=False, stop=True)
                nc.scalar.copy(out=node0[:, cols], in_=half_sum[:])
            nc.sync.dma_start(out=out[0].rearrange("b c h w -> (b c) (h w)"), in_=node0[:])

        upper = slice(PAIRS_OF[UPPER][0], PAIRS_OF[UPPER][-1] + 1)
        n_upper = len(PAIRS_OF[UPPER])
        sums = psum.tile([P, n_upper, len(SUM_PARTS), SUM_COLS], F32, tag="sums", bufs=SUM_BANKS)

        def sum_pixels(part):
            for pair in PAIRS_OF[UPPER]:
                multiply(
                    sums[:, pair, part, :], pair,
                    [(k, first, SUM_COLS) for k in SUM_PARTS[part] for first in range(0, N_TILE, SUM_COLS)],
                )

        pilot = keep.tile([P, n_upper], F32)
        minus_pilot = keep.tile([P, n_upper], F32)
        minus_pilot_gamma = keep.tile([P, n_upper], F32)
        squares = keep.tile([P, n_upper, len(pixel_tiles)], F32)

        def take_pilot():
            for pair in PAIRS_OF[UPPER]:
                unused = results.tile([P, N_TILE], BF16)
                nc.scalar.activation(
                    out=unused[:, 0:SUM_COLS], in_=y_banks[(pair, 0)][:, 0:SUM_COLS], func=ACT.Copy,
                    scale=1.0 / SUM_COLS, accum_out=pilot[:, pair : pair + 1],
                )
            nc.scalar.activation(
                out=minus_pilot[:], in_=pilot[:], func=ACT.Copy, scale=-1.0 / (len(SUM_PARTS) * SUM_COLS)
            )

        def take_squares(k):
            for pair in PAIRS_OF[UPPER]:
                unused = results.tile([P, N_TILE], BF16)
                nc.scalar.activation(
                    out=unused[:], in_=y_banks[(pair, k)][:], func=ACT.Square, scale=-1.0,
                    bias=pilot[:, pair : pair + 1], accum_out=squares[:, pair, k : k + 1],
                )

        tuples = keep.tile([P, last * TUPLE + STATS], F32)
        nc.vector.memset(tuples[:], float(N_TILE))

        def take_tuple(k):
            (pair,) = PAIRS_OF[LOWER]
            mean = tuples[:, k * TUPLE + 1 : k * TUPLE + 2]
            unused = results.tile([P, N_TILE], BF16)
            nc.scalar.activation(
                out=unused[:], in_=y_banks[(pair, k)][:], func=ACT.Copy, scale=1.0 / N_TILE, accum_out=mean
            )
            unused = results.tile([P, N_TILE], BF16)
            nc.scalar.activation(
                out=unused[:], in_=y_banks[(pair, k)][:], func=ACT.Square, scale=-1.0, bias=mean,
                accum_out=tuples[:, k * TUPLE + 2 : k * TUPLE + 3],
            )

        mean_less_pilot = keep.tile([P, n_upper], F32)
        square_sum = keep.tile([P, n_upper], F32)
        variance = keep.tile([P, n_upper], F32)
        mean_var = keep.tile([P, 2], F32)
        minus_mean_gamma = keep.tile([P, N_PAIRS], F32)
        inv_std = keep.tile([P, N_PAIRS], F32)
        gain = keep.tile([P, N_PAIRS], F32)
        shift = keep.tile([P, N_PAIRS], F32)

        mean_parts = keep.tile([P, n_upper, 2], F32)

        def take_mean_of_sums():
            width = len(SUM_PARTS) * SUM_COLS
            for pair in PAIRS_OF[UPPER]:
                unused = results.tile([P, N_TILE], BF16)
                nc.scalar.activation(
                    out=unused[:, 0:width], in_=sums[:, pair].rearrange("p s w -> p (s w)"),
                    func=ACT.Identity, scale=1.0 / COUNT, bias=minus_pilot[:, pair : pair + 1],
                    accum_out=mean_parts[:, pair, 0:1],
                )

        def take_mean_of_last():
            for pair in PAIRS_OF[UPPER]:
                unused = results.tile([P, N_TILE], BF16)
                nc.scalar.activation(
                    out=unused[:], in_=y_banks[(pair, last)][:], func=ACT.Copy, scale=1.0 / COUNT,
                    accum_out=mean_parts[:, pair, 1:2],
                )

        def pilot_and_gamma():
            nc.vector.scalar_tensor_tensor(
                out=minus_pilot_gamma[:], in0=pilot[:], scalar=-1.0, in1=half_affine[:, upper],
                op0=ALU.mult, op1=ALU.mult,
            )

        def upper_mean_and_variance():
            nc.vector.tensor_reduce(out=mean_less_pilot[:], in_=mean_parts[:], axis=mybir.AxisListType.X, op=ALU.add)
            nc.vector.tensor_reduce(out=square_sum[:], in_=squares[:], axis=mybir.AxisListType.X, op=ALU.add)
            nc.vector.scalar_tensor_tensor(
                out=variance[:], in0=mean_less_pilot[:], scalar=-1.0, in1=mean_less_pilot[:],
                op0=ALU.mult, op1=ALU.mult,
            )
            nc.vector.scalar_tensor_tensor(
                out=minus_mean_gamma[:, upper], in0=mean_less_pilot[:], scalar=-1.0, in1=half_affine[:, upper],
                op0=ALU.mult, op1=ALU.mult,
            )
            nc.vector.scalar_tensor_tensor(
                out=variance[:], in0=square_sum[:], scalar=1.0 / COUNT, in1=variance[:],
                op0=ALU.mult, op1=ALU.add,
            )
            nc.vector.tensor_tensor(
                out=minus_mean_gamma[:, upper], in0=minus_mean_gamma[:, upper], in1=minus_pilot_gamma[:], op=ALU.add
            )

        def lower_mean_and_variance():
            (pair,) = PAIRS_OF[LOWER]
            one = slice(pair, pair + 1)
            nc.vector.bn_aggr(out=mean_var[:], in_=tuples[:])
            nc.vector.scalar_tensor_tensor(
                out=minus_mean_gamma[:, one], in0=mean_var[:, 0:1], scalar=-1.0, in1=half_affine[:, one],
                op0=ALU.mult, op1=ALU.mult,
            )

        def gain_and_shift(product):
            pairs = PAIRS_OF[product]
            these = slice(pairs[0], pairs[-1] + 1)
            nc.scalar.activation(
                out=inv_std[:, these], in_=variance[:] if product == UPPER else mean_var[:, 1:2],
                func=ACT.Abs_reciprocal_sqrt, bias=eps[:],
            )
            for pair in pairs:
                one = slice(pair, pair + 1)
                nc.scalar.activation(out=gain[:, one], in_=half_affine[:, one], func=ACT.Copy, scale=inv_std[:, one])
                nc.scalar.activation(
                    out=shift[:, one], in_=minus_mean_gamma[:, one], func=ACT.Identity, scale=inv_std[:, one],
                    bias=half_affine[:, N_PAIRS + pair : N_PAIRS + pair + 1],
                )

        half_relus = {}

        def normalise(pair, k, tiles):
            half_relu = results.tile([P, 2 * N_TILE], F32)
            for i in range(tiles):
                nc.scalar.activation(
                    out=half_relu[:, i * N_TILE : (i + 1) * N_TILE], in_=y_banks[(pair, k + i)][:], func=ACT.Relu,
                    bias=shift[:, pair : pair + 1], scale=gain[:, pair : pair + 1],
                )
            half_relus[(pair, k)] = half_relu

        def add_node(pair, k, tiles):
            b, wt = pixel_tiles[k]
            cols = slice(wt * N_TILE, (wt + tiles) * N_TILE)
            result = results.tile([P, 2 * N_TILE], F32)
            nc.vector.scalar_tensor_tensor(
                out=result[:, 0 : tiles * N_TILE], in0=p_pairs[:, pair, b, cols], scalar=0.5,
                in1=half_relus[(pair, k)][:, 0 : tiles * N_TILE], op0=ALU.mult, op1=ALU.add,
            )
            for half in range(2):
                nc.sync.dma_start(
                    out=out[1 + 2 * pair + half, b].rearrange("c h w -> c (h w)")[:, cols],
                    in_=result[half:P:2, 0 : tiles * N_TILE],
                )

        regroup_pixels(nc.vector.tensor_copy, 0, 0, 0, N_TILE - 128)
        regroup_pixels(nc.scalar.copy, 0, 0, N_TILE - 128, N_TILE)
        regroup_pixels(nc.scalar.copy, 0, 1, 0, N_TILE - 128)
        nc.gpsimd.tensor_scalar(
            out=xp_grouped[:, 0, 1, N_TILE - 128 : N_TILE, :],
            in0=xp_rows[(0, 1)][:, :, N_TILE - 128 :].rearrange("p t w -> p w t"),
            scalar1=1.0, scalar2=0.0, op0=ALU.mult, op1=ALU.add,
        )
        regroup_on_gpsimd(1, 0, pieces=2)
        regroup(nc.scalar.copy, 1, 1)
        for product in (UPPER, LOWER):
            weave(woven_words, loaded_words, product)
        for product in (UPPER, LOWER):
            weave(woven_scales, loaded_scales, product)
        nc.gpsimd.tensor_copy(
            out=affine_woven[:].rearrange("p (c h) -> p c h", h=2),
            in_=affine_rows[:].rearrange("p (h c) -> p c h", h=2),
        )
        regroup(nc.scalar.copy, 2, 0)
        regroup(nc.scalar.copy, 2, 1)
        regroup(nc.scalar.copy, 3, 0)

        weigh(UPPER, 0, 0)
        weigh(LOWER, 0, 0)
        weigh(UPPER, 0, 1)
        spread_attention(*units[ATT_BANKS])
        weigh(LOWER, 0, 1)
        spread_attention(*units[ATT_BANKS + 1])
        quantise(*units[0])
        for pair in PAIRS_OF[UPPER]:
            convolve(pair, 0)
        take_pilot()
        take_squares(0)
        regroup_pixels(nc.scalar.copy, 3, 1, 0, N_TILE - 256)

        kept_tiles = (2, 3)
        (lower_pair,) = PAIRS_OF[LOWER]
        upper_runs = [(pair, k, PIXEL_TILES) for k in range(0, len(pixel_tiles), PIXEL_TILES) for pair in PAIRS_OF[UPPER]]

        def convolve_and_normalise(pair, k, tiles):
            for i in range(tiles):
                convolve(pair, k + i)
            normalise(pair, k, tiles)

        for n in range(2, len(units)):
            weigh(units[n][0], units[n][1], 0)
            product, k = units[n - 1]
            quantise(product, k)
            if n == 7:
                convolve_and_normalise(*upper_runs[0])
                convolve_and_normalise(*upper_runs[1])
                average_node0()
            for pair in PAIRS_OF[product]:
                if product == LOWER and k in kept_tiles:
                    convolve(pair, k, "att", ATT_BANKS)
                else:
                    convolve(pair, k)
            if product == UPPER:
                take_squares(k)
            else:
                take_tuple(k)
            if n == 4:
                regroup_pixels(nc.vector.tensor_copy, 3, 1, N_TILE - 256, N_TILE)
            weigh(units[n][0], units[n][1], 1)
            if n + ATT_BANKS < len(units):
                spread_attention(*units[n + ATT_BANKS])
            if n == 3:
                sum_pixels(0)
            if n == 4:
                sum_pixels(1)
                affine_ps = psum.tile([P, P], BF16, tag="y", bufs=Y_BANKS)
                nc.tensor.transpose(out=affine_ps[:], in_=affine_woven[:], identity=identity[:])
                nc.scalar.activation(out=half_affine[:], in_=affine_ps[:, 0 : 2 * N_PAIRS], func=ACT.Copy, scale=0.5)
                take_mean_of_sums()
            if n == 5:
                take_mean_of_last()
            if n == 6:
                pilot_and_gamma()
                upper_mean_and_variance()
                gain_and_shift(UPPER)
        convolve_and_normalise(*upper_runs[2])
        quantise(*units[-1])
        add_node(*upper_runs[0])
        convolve(lower_pair, last, "att", ATT_BANKS)
        add_node(*upper_runs[1])
        nc.vector.bn_stats(out=tuples[:, last * TUPLE : last * TUPLE + STATS], in_=y_banks[(lower_pair, last)][:])
        lower_mean_and_variance()
        convolve_and_normalise(*upper_runs[3])
        gain_and_shift(LOWER)
        add_node(*upper_runs[2])
        add_node(*upper_runs[3])

        convolve_and_normalise(lower_pair, 0, PIXEL_TILES)
        add_node(lower_pair, 0, PIXEL_TILES)
        for k in kept_tiles:
            normalise(lower_pair, k, 1)
            add_node(lower_pair, k, 1)
